import numpy as np
import ml_dtypes


def mxq(x, axis, fmt="e4m3"):
    dtype, down = {"e4m3": (ml_dtypes.float8_e4m3fn, 7), "e5m2": (ml_dtypes.float8_e5m2, 14)}[fmt]
    v = np.moveaxis(np.asarray(x, np.float32).astype(ml_dtypes.bfloat16).astype(np.float64), axis, -1)
    blocks = v.reshape(v.shape[:-1] + (-1, 32))
    amax = np.abs(blocks).max(-1, keepdims=True)
    byte = np.maximum(np.where(amax > 0, np.frexp(amax)[1] - 1 + 127, 0) - down, 1)
    scale = np.exp2(byte - 127.0)
    codes = (blocks / scale).astype(np.float32).astype(dtype).astype(np.float64)
    return np.moveaxis((codes * scale).reshape(v.shape), -1, axis)


WIDE = False


def mx_kscale(k):
    if not WIDE:
        return np.ones(k)
    levels = np.array([20, -20, 10, -10, 0])
    a = np.random.permutation(np.resize(levels, k // 512 * 4)).reshape(k // 512, 4)
    idx = np.arange(k)
    return np.exp2(a[idx // 512, idx % 128 // 32])


BF16 = ml_dtypes.bfloat16


def bf(x):
    return np.asarray(x, np.float32).astype(BF16)


def f64(x):
    return np.asarray(x).astype(np.float64)


B, NI, NK, NJ, C_Z, C_H = 1, 512, 512, 512, 128, 8
EPS = 1e-5
KEEP = 0.85
GSCALE = 8.0


def norm_stats(a_gated, b_gated, mask_ik, mask_kj):
    a = mask_ik[..., None] * a_gated
    b = mask_kj[..., None] * b_gated
    x = (a.transpose(0, 3, 1, 2) @ b.transpose(0, 3, 1, 2)).transpose(0, 2, 3, 1)
    mu = x.mean(-1, keepdims=True)
    var = ((x - mu) ** 2).mean(-1, keepdims=True)
    r = 1.0 / np.sqrt(var + EPS)
    return (x - mu) * r, r[..., 0]


def setup_inputs():
    s = mx_kscale(NJ)[None, None, :, None]
    a = bf(np.random.standard_normal((B, NI, NK, C_H)) * 0.55)
    b0 = bf(np.random.standard_normal((B, NK, NJ, C_H)) * 0.55)
    mik = bf(np.random.random((B, NI, NK)) < KEEP)
    mkj = bf(np.random.random((B, NK, NJ)) < KEEP)
    w = bf(1.0 + 0.1 * np.random.standard_normal(C_H))
    c = bf(0.1 * np.random.standard_normal(C_H))
    g = bf(np.random.standard_normal((B, NI, NJ, C_H)) * np.exp2(np.random.randint(-12, 1, (B, NI, NJ, 1))) * GSCALE * s)
    xh, r = norm_stats(f64(a), f64(b0), f64(mik), f64(mkj))
    return {"a_gated": a,
            "b_gated": bf(f64(b0) / s),
            "mask_ik": mik,
            "mask_kj": mkj,
            "ln_out_w": w,
            "ln_out_b": c,
            "xhat": np.asarray(xh, np.float32),
            "rstd": np.asarray(r, np.float32),
            "grad_out": g}


def reference(a_gated, b_gated, mask_ik, mask_kj, ln_out_w, ln_out_b, xhat, rstd, grad_out):
    xh = f64(xhat)
    gw = f64(grad_out) * f64(ln_out_w)
    m1 = gw.mean(-1, keepdims=True)
    m2 = (gw * xh).mean(-1, keepdims=True)
    dx = f64(rstd)[..., None] * (gw - m1 - xh * m2)
    b = f64(mask_kj)[..., None] * f64(b_gated)
    dxt = dx.transpose(0, 3, 1, 2)
    bt = b.transpose(0, 3, 1, 2)
    da = mxq(dxt, 3, "e5m2") @ mxq(bt, 3, "e4m3").transpose(0, 1, 3, 2)
    return f64(mask_ik)[..., None] * da.transpose(0, 2, 3, 1)

@@ -1,0 +1,153 @@
+from contextlib import ExitStack
+
+import concourse.mybir as mybir
+from concourse.masks import make_identity
+
+F32 = mybir.dt.float32
+BF16 = mybir.dt.bfloat16
+U32 = mybir.dt.uint32
+U8 = mybir.dt.uint8
+E4M3X4 = mybir.dt.float8_e4m3fn_x4
+E5M2X4 = mybir.dt.float8_e5m2_x4
+MULT = mybir.AluOpType.mult
+ADD = mybir.AluOpType.add
+SUB = mybir.AluOpType.subtract
+AXIS_X = mybir.AxisListType.X
+
+P = 128
+PACK = 4
+N = 512
+D = 8
+BLOCKS = N // P
+PAIRS = D // 2
+
+FLOPS = 2 * D * N * N * N
+BYTES = N * N * D * (2 + 4 + 2 + 4) + N * N * (4 + 2 + 2) + D * 2
+
+
+def transpose_channel_pairs(nc, psum, ident, rows, grouped):
+    words = rows.bitcast(F32).rearrange("p (t q e) -> p t e q", t=PACK, e=PAIRS)
+    for e in range(PAIRS):
+        flipped = psum.tile([P, PACK * P], F32, tag="flipped")
+        for t in range(PACK):
+            nc.tensor.transpose(flipped[:, t * P : (t + 1) * P], words[:, t, e, :], ident)
+        nc.scalar.copy(
+            out=grouped[:, 2 * e : 2 * e + 2, :, :],
+            in_=flipped[:].bitcast(BF16).rearrange("p (t r h) -> p h r t", t=PACK, h=2),
+        )
+
+
+def tile_trianglemultiplicativeupdate_pa_v_kernel(
+    tc, a_gated, b_gated, mask_ik, mask_kj, ln_out_w, ln_out_b, xhat, rstd, grad_out, out
+):
+    nc = tc.nc
+    b_rows = b_gated.rearrange("n k j d -> (n k) (j d)")
+    g_rows = grad_out.rearrange("n i j d -> (n i) (j d)")
+    xh_rows = xhat.rearrange("n i j d -> (n i) (j d)")
+    out_rows = out.rearrange("n i k d -> (n i) (k d)")
+    r_rows = rstd.rearrange("n i j -> (n i) j")
+    mik_rows = mask_ik.rearrange("n i k -> (n i) k")
+    mkj_rows = mask_kj.rearrange("n k j -> (n k) j")
+
+    with ExitStack() as stack:
+        const = stack.enter_context(tc.tile_pool(name="const", bufs=1))
+        keep = stack.enter_context(tc.tile_pool(name="keep", bufs=1))
+        loads = stack.enter_context(tc.tile_pool(name="loads", bufs=2))
+        work = stack.enter_context(tc.tile_pool(name="work", bufs=1))
+        quant = stack.enter_context(tc.tile_pool(name="quant", bufs=2))
+        psum = stack.enter_context(tc.psum_pool(name="psum", bufs=4))
+
+        ident = const.tile([P, P], F32)
+        make_identity(nc, ident[:])
+        w_all = const.tile([P, D], BF16)
+        nc.sync.dma_start(out=w_all[:], in_=ln_out_w.partition_broadcast(P))
+
+        b_codes = keep.tile([P, D, N], U32, align_bytes=64)
+        b_scales = keep.tile([P, D, N], U8, align_bytes=64)
+
+        with tc.tile_pool(name="b_tmp", bufs=2) as b_tmp, tc.tile_pool(name="b_grp", bufs=1) as b_grp:
+            b_grouped = b_grp.tile([P, D, N, PACK], BF16, align_bytes=64)
+            for kb in range(BLOCKS):
+                k_rows = slice(kb * P, (kb + 1) * P)
+                b_nat = b_tmp.tile([P, N * D], BF16)
+                nc.sync.dma_start(out=b_nat[:], in_=b_rows[k_rows, :])
+                mkj = b_tmp.tile([P, N], BF16)
+                nc.sync.dma_start(out=mkj[:], in_=mkj_rows[k_rows, :])
+                b_masked = b_tmp.tile([P, N * D], BF16)
+                nc.vector.tensor_tensor(
+                    out=b_masked[:].rearrange("p (j d) -> p j d", d=D),
+                    in0=b_nat[:].rearrange("p (j d) -> p j d", d=D),
+                    in1=mkj[:].unsqueeze(2).to_broadcast([P, N, D]),
+                    op=MULT,
+                )
+                transpose_channel_pairs(nc, psum, ident[:], b_masked[:], b_grouped[:, :, k_rows, :])
+            for d in range(D):
+                nc.vector.quantize_mx(
+                    out=b_codes[:, d, :].bitcast(E4M3X4),
+                    scales=b_scales[:, d, :],
+                    in_=b_grouped[:, d, :, :].rearrange("p k t -> p (k t)"),
+                )
+
+        outs = stack.enter_context(tc.tile_pool(name="outs", bufs=1))
+
+        for ib in range(BLOCKS):
+            i_rows = slice(ib * P, (ib + 1) * P)
+            g_nat = loads.tile([P, N, D], BF16)
+            nc.sync.dma_start(out=g_nat[:].rearrange("p j d -> p (j d)"), in_=g_rows[i_rows, :])
+            xh = loads.tile([P, N, D], F32)
+            nc.sync.dma_start(out=xh[:].rearrange("p j d -> p (j d)"), in_=xh_rows[i_rows, :])
+            r = loads.tile([P, N], F32)
+            nc.sync.dma_start(out=r[:], in_=r_rows[i_rows, :])
+            mik = loads.tile([P, N], BF16)
+            nc.sync.dma_start(out=mik[:], in_=mik_rows[i_rows, :])
+
+            gw = work.tile([P, N, D], F32)
+            nc.vector.tensor_tensor(out=gw[:], in0=g_nat[:], in1=w_all[:].unsqueeze(1).to_broadcast([P, N, D]), op=MULT)
+            prod = work.tile([P, N, D], F32)
+            nc.vector.tensor_tensor(out=prod[:], in0=gw[:], in1=xh[:], op=MULT)
+            s1 = work.tile([P, N], F32)
+            nc.vector.tensor_reduce(out=s1[:], in_=gw[:], axis=AXIS_X, op=ADD)
+            s2 = work.tile([P, N], F32)
+            nc.vector.tensor_reduce(out=s2[:], in_=prod[:], axis=AXIS_X, op=ADD)
+            m1r = work.tile([P, N], F32)
+            nc.vector.scalar_tensor_tensor(out=m1r[:], in0=s1[:], scalar=1.0 / D, in1=r[:], op0=MULT, op1=MULT)
+            m2r = work.tile([P, N], F32)
+            nc.vector.scalar_tensor_tensor(out=m2r[:], in0=s2[:], scalar=1.0 / D, in1=r[:], op0=MULT, op1=MULT)
+            part = work.tile([P, N, D], F32, tag="prod")
+            nc.vector.tensor_tensor(out=part[:], in0=xh[:], in1=m2r[:].unsqueeze(2).to_broadcast([P, N, D]), op=MULT)
+            gwr = work.tile([P, N, D], F32)
+            nc.vector.tensor_tensor(out=gwr[:], in0=gw[:], in1=r[:].unsqueeze(2).to_broadcast([P, N, D]), op=MULT)
+            diff = work.tile([P, N, D], F32, tag="gw")
+            nc.vector.tensor_tensor(out=diff[:], in0=gwr[:], in1=part[:], op=SUB)
+            dx_nat = work.tile([P, N, D], BF16)
+            nc.vector.tensor_tensor(out=dx_nat[:], in0=diff[:], in1=m1r[:].unsqueeze(2).to_broadcast([P, N, D]), op=SUB)
+
+            dx_grouped = quant.tile([P, D, P, PACK], BF16, align_bytes=64)
+            transpose_channel_pairs(nc, psum, ident[:], dx_nat[:].rearrange("p j d -> p (j d)"), dx_grouped[:])
+            dx_codes = quant.tile([P, D * P], U32, align_bytes=64)
+            dx_scales = quant.tile([P, D * P], U8, align_bytes=64)
+            nc.vector.quantize_mx(
+                out=dx_codes[:].bitcast(E5M2X4),
+                scales=dx_scales[:],
+                in_=dx_grouped[:].rearrange("p d i t -> p (d i t)"),
+            )
+
+            planes = outs.tile([P, D, N], F32)
+            for d in range(D):
+                i_cols = slice(d * P, (d + 1) * P)
+                acc = psum.tile([P, N], F32, tag="acc")
+                nc.tensor.matmul_mx(
+                    out=acc[:],
+                    lhsT=dx_codes[:, i_cols].bitcast(E5M2X4),
+                    lhsT_scale=dx_scales[:, i_cols],
+                    rhs=b_codes[:, d, :].bitcast(E4M3X4),
+                    rhs_scale=b_scales[:, d, :],
+                    start=True,
+                    stop=True,
+                )
+                nc.vector.tensor_tensor(out=planes[:, d, :], in0=acc[:], in1=mik[:], op=MULT)
+            out_sb = outs.tile([P, N, D], F32)
+            for half in range(2):
+                d_half = slice(half * 4, half * 4 + 4)
+                nc.scalar.copy(out=out_sb[:, :, d_half], in_=planes[:, d_half, :].rearrange("p d k -> p k d"))
+            nc.sync.dma_start(out=out_rows[i_rows, :], in_=out_sb[:].rearrange("p k d -> p (k d)"))

@@ -110,20 +110,23 @@ def tile_trianglemultiplicativeupdate_pa_v_kernel(
             s2 = work.tile([P, N], F32)
             nc.vector.tensor_reduce(out=s2[:], in_=prod[:], axis=AXIS_X, op=ADD)
             m1r = work.tile([P, N], F32)
-            nc.vector.scalar_tensor_tensor(out=m1r[:], in0=s1[:], scalar=1.0 / D, in1=r[:], op0=MULT, op1=MULT)
+            nc.vector.scalar_tensor_tensor(out=m1r[:], in0=s1[:], scalar=-1.0 / D, in1=r[:], op0=MULT, op1=MULT)
             m2r = work.tile([P, N], F32)
-            nc.vector.scalar_tensor_tensor(out=m2r[:], in0=s2[:], scalar=1.0 / D, in1=r[:], op0=MULT, op1=MULT)
+            nc.vector.scalar_tensor_tensor(out=m2r[:], in0=s2[:], scalar=-1.0 / D, in1=r[:], op0=MULT, op1=MULT)
             part = work.tile([P, N, D], F32, tag="prod")
             nc.vector.tensor_tensor(out=part[:], in0=xh[:], in1=m2r[:].unsqueeze(2).to_broadcast([P, N, D]), op=MULT)
             gwr = work.tile([P, N, D], F32)
             nc.vector.tensor_tensor(out=gwr[:], in0=gw[:], in1=r[:].unsqueeze(2).to_broadcast([P, N, D]), op=MULT)
-            diff = work.tile([P, N, D], F32, tag="gw")
-            nc.vector.tensor_tensor(out=diff[:], in0=gwr[:], in1=part[:], op=SUB)
-            dx_nat = work.tile([P, N, D], BF16)
-            nc.vector.tensor_tensor(out=dx_nat[:], in0=diff[:], in1=m1r[:].unsqueeze(2).to_broadcast([P, N, D]), op=SUB)
 
             dx_grouped = quant.tile([P, D, P, PACK], BF16, align_bytes=64)
-            transpose_channel_pairs(nc, psum, ident[:], dx_nat[:].rearrange("p j d -> p (j d)"), dx_grouped[:])
+            for d in range(D):
+                dx_t = psum.tile([P, PACK * P], F32, tag="flipped")
+                for t in range(PACK):
+                    j_cols = slice(t * P, (t + 1) * P)
+                    nc.tensor.matmul(out=dx_t[:, j_cols], lhsT=gwr[:, j_cols, d], rhs=ident[:], is_transpose=True, start=True, stop=False)
+                    nc.tensor.matmul(out=dx_t[:, j_cols], lhsT=part[:, j_cols, d], rhs=ident[:], is_transpose=True, start=False, stop=False)
+                    nc.tensor.matmul(out=dx_t[:, j_cols], lhsT=m1r[:, j_cols], rhs=ident[:], is_transpose=True, start=False, stop=True)
+                nc.scalar.copy(out=dx_grouped[:, d, :, :], in_=dx_t[:].rearrange("p (t i) -> p i t", t=PACK))
             dx_codes = quant.tile([P, D * P], U32, align_bytes=64)
             dx_scales = quant.tile([P, D * P], U8, align_bytes=64)
             nc.vector.quantize_mx(

@@ -10,31 +10,27 @@ U8 = mybir.dt.uint8
 E4M3X4 = mybir.dt.float8_e4m3fn_x4
 E5M2X4 = mybir.dt.float8_e5m2_x4
 MULT = mybir.AluOpType.mult
-ADD = mybir.AluOpType.add
 SUB = mybir.AluOpType.subtract
-AXIS_X = mybir.AxisListType.X
 
 P = 128
 PACK = 4
 N = 512
 D = 8
+HALF = D // 2
 BLOCKS = N // P
 PAIRS = D // 2
+
+FIRST_B_SLOT = 9
+B_SLOT_STEP = 3
+FIRST_MX_SLOT = FIRST_B_SLOT + B_SLOT_STEP * BLOCKS
+MX_RUN = 2
 
 FLOPS = 2 * D * N * N * N
 BYTES = N * N * D * (2 + 4 + 2 + 4) + N * N * (4 + 2 + 2) + D * 2
 
 
-def transpose_channel_pairs(nc, psum, ident, rows, grouped):
-    words = rows.bitcast(F32).rearrange("p (t q e) -> p t e q", t=PACK, e=PAIRS)
-    for e in range(PAIRS):
-        flipped = psum.tile([P, PACK * P], F32, tag="flipped")
-        for t in range(PACK):
-            nc.tensor.transpose(flipped[:, t * P : (t + 1) * P], words[:, t, e, :], ident)
-        nc.scalar.copy(
-            out=grouped[:, 2 * e : 2 * e + 2, :, :],
-            in_=flipped[:].bitcast(BF16).rearrange("p (t r h) -> p h r t", t=PACK, h=2),
-        )
+def block_cols(t):
+    return slice(t * P, (t + 1) * P)
 
 
 def tile_trianglemultiplicativeupdate_pa_v_kernel(
@@ -50,107 +46,223 @@ def tile_trianglemultiplicativeupdate_pa_v_kernel(
     mkj_rows = mask_kj.rearrange("n k j -> (n k) j")
 
     with ExitStack() as stack:
+        stack.enter_context(tc.manual_schedule())
         const = stack.enter_context(tc.tile_pool(name="const", bufs=1))
-        keep = stack.enter_context(tc.tile_pool(name="keep", bufs=1))
-        loads = stack.enter_context(tc.tile_pool(name="loads", bufs=2))
-        work = stack.enter_context(tc.tile_pool(name="work", bufs=1))
-        quant = stack.enter_context(tc.tile_pool(name="quant", bufs=2))
-        psum = stack.enter_context(tc.psum_pool(name="psum", bufs=4))
+        every = stack.enter_context(tc.tile_pool(name="every", bufs=BLOCKS))
+        two = stack.enter_context(tc.tile_pool(name="two", bufs=2))
+        one = stack.enter_context(tc.tile_pool(name="one", bufs=1))
+        psum = stack.enter_context(tc.psum_pool(name="psum", bufs=2))
+
+        tiles = {}
 
         ident = const.tile([P, P], F32)
         make_identity(nc, ident[:])
-        w_all = const.tile([P, D], BF16)
-        nc.sync.dma_start(out=w_all[:], in_=ln_out_w.partition_broadcast(P))
+        w_bf = const.tile([P, D], BF16)
+        nc.scalar.dma_start(out=w_bf[:], in_=ln_out_w.partition_broadcast(P))
+        w_all = const.tile([P, D], F32)
+        nc.vector.tensor_copy(out=w_all[:], in_=w_bf[:])
+        b_codes = const.tile([P, D, N], U32, align_bytes=64)
+        b_scales = const.tile([P, D, N], U8, align_bytes=64)
 
-        b_codes = keep.tile([P, D, N], U32, align_bytes=64)
-        b_scales = keep.tile([P, D, N], U8, align_bytes=64)
+        def flip(out_cols, in_cols, start=True, stop=True):
+            nc.tensor.matmul(out=out_cols, lhsT=in_cols, rhs=ident[:], is_transpose=True, start=start, stop=stop)
 
-        with tc.tile_pool(name="b_tmp", bufs=2) as b_tmp, tc.tile_pool(name="b_grp", bufs=1) as b_grp:
-            b_grouped = b_grp.tile([P, D, N, PACK], BF16, align_bytes=64)
-            for kb in range(BLOCKS):
-                k_rows = slice(kb * P, (kb + 1) * P)
-                b_nat = b_tmp.tile([P, N * D], BF16)
-                nc.sync.dma_start(out=b_nat[:], in_=b_rows[k_rows, :])
-                mkj = b_tmp.tile([P, N], BF16)
-                nc.sync.dma_start(out=mkj[:], in_=mkj_rows[k_rows, :])
-                b_masked = b_tmp.tile([P, N * D], BF16)
-                nc.vector.tensor_tensor(
-                    out=b_masked[:].rearrange("p (j d) -> p j d", d=D),
-                    in0=b_nat[:].rearrange("p (j d) -> p j d", d=D),
-                    in1=mkj[:].unsqueeze(2).to_broadcast([P, N, D]),
-                    op=MULT,
-                )
-                transpose_channel_pairs(nc, psum, ident[:], b_masked[:], b_grouped[:, :, k_rows, :])
-            for d in range(D):
-                nc.vector.quantize_mx(
-                    out=b_codes[:, d, :].bitcast(E4M3X4),
-                    scales=b_scales[:, d, :],
-                    in_=b_grouped[:, d, :, :].rearrange("p k t -> p (k t)"),
-                )
-
-        outs = stack.enter_context(tc.tile_pool(name="outs", bufs=1))
-
-        for ib in range(BLOCKS):
-            i_rows = slice(ib * P, (ib + 1) * P)
-            g_nat = loads.tile([P, N, D], BF16)
-            nc.sync.dma_start(out=g_nat[:].rearrange("p j d -> p (j d)"), in_=g_rows[i_rows, :])
-            xh = loads.tile([P, N, D], F32)
-            nc.sync.dma_start(out=xh[:].rearrange("p j d -> p (j d)"), in_=xh_rows[i_rows, :])
-            r = loads.tile([P, N], F32)
+        def load_block(b):
+            i_rows = block_cols(b)
+            g_nat = two.tile([P, N * D], BF16, tag="g_nat")
+            nc.sync.dma_start(out=g_nat[:], in_=g_rows[i_rows, :])
+            r = two.tile([P, N], F32, tag="r")
             nc.sync.dma_start(out=r[:], in_=r_rows[i_rows, :])
-            mik = loads.tile([P, N], BF16)
+            xh = two.tile([P, N, D], F32, tag="xh")
+            nc.sync.dma_start(out=xh[:].rearrange("p j d -> p (j d)"), in_=xh_rows[i_rows, :])
+            mik = every.tile([P, N], BF16, tag="mik")
             nc.sync.dma_start(out=mik[:], in_=mik_rows[i_rows, :])
+            tiles["g_nat", b], tiles["r", b], tiles["xh", b], tiles["mik", b] = g_nat, r, xh, mik
 
-            gw = work.tile([P, N, D], F32)
-            nc.vector.tensor_tensor(out=gw[:], in0=g_nat[:], in1=w_all[:].unsqueeze(1).to_broadcast([P, N, D]), op=MULT)
-            prod = work.tile([P, N, D], F32)
-            nc.vector.tensor_tensor(out=prod[:], in0=gw[:], in1=xh[:], op=MULT)
-            s1 = work.tile([P, N], F32)
-            nc.vector.tensor_reduce(out=s1[:], in_=gw[:], axis=AXIS_X, op=ADD)
-            s2 = work.tile([P, N], F32)
-            nc.vector.tensor_reduce(out=s2[:], in_=prod[:], axis=AXIS_X, op=ADD)
-            m1r = work.tile([P, N], F32)
-            nc.vector.scalar_tensor_tensor(out=m1r[:], in0=s1[:], scalar=-1.0 / D, in1=r[:], op0=MULT, op1=MULT)
-            m2r = work.tile([P, N], F32)
-            nc.vector.scalar_tensor_tensor(out=m2r[:], in0=s2[:], scalar=-1.0 / D, in1=r[:], op0=MULT, op1=MULT)
-            part = work.tile([P, N, D], F32, tag="prod")
-            nc.vector.tensor_tensor(out=part[:], in0=xh[:], in1=m2r[:].unsqueeze(2).to_broadcast([P, N, D]), op=MULT)
-            gwr = work.tile([P, N, D], F32)
-            nc.vector.tensor_tensor(out=gwr[:], in0=gw[:], in1=r[:].unsqueeze(2).to_broadcast([P, N, D]), op=MULT)
+        def flip_rstd(b):
+            r_ps = psum.tile([P, N], F32, tag="wide")
+            for t in range(PACK):
+                flip(r_ps[:, block_cols(t)], tiles["r", b][:, block_cols(t)])
+            r_t = two.tile([P, N], F32, tag="r_t")
+            nc.scalar.copy(out=r_t[:], in_=r_ps[:])
+            tiles["r_t", b] = r_t
 
-            dx_grouped = quant.tile([P, D, P, PACK], BF16, align_bytes=64)
-            for d in range(D):
-                dx_t = psum.tile([P, PACK * P], F32, tag="flipped")
+        def flip_in(b, d):
+            if d % 2 == 0:
+                g_words = tiles["g_nat", b][:].bitcast(F32).rearrange("p (t q e) -> p t e q", t=PACK, e=PAIRS)
+                g_t = psum.tile([P, N], F32, tag="g_t")
                 for t in range(PACK):
-                    j_cols = slice(t * P, (t + 1) * P)
-                    nc.tensor.matmul(out=dx_t[:, j_cols], lhsT=gwr[:, j_cols, d], rhs=ident[:], is_transpose=True, start=True, stop=False)
-                    nc.tensor.matmul(out=dx_t[:, j_cols], lhsT=part[:, j_cols, d], rhs=ident[:], is_transpose=True, start=False, stop=False)
-                    nc.tensor.matmul(out=dx_t[:, j_cols], lhsT=m1r[:, j_cols], rhs=ident[:], is_transpose=True, start=False, stop=True)
-                nc.scalar.copy(out=dx_grouped[:, d, :, :], in_=dx_t[:].rearrange("p (t i) -> p i t", t=PACK))
-            dx_codes = quant.tile([P, D * P], U32, align_bytes=64)
-            dx_scales = quant.tile([P, D * P], U8, align_bytes=64)
+                    flip(g_t[:, block_cols(t)], g_words[:, t, d // 2, :])
+                tiles["g_t", b, d // 2] = g_t
+            x_t = psum.tile([P, N], F32, tag="x_t")
+            for t in range(PACK):
+                flip(x_t[:, block_cols(t)], tiles["xh", b][:, block_cols(t), d])
+            tiles["x_t", b, d] = x_t
+
+        def scale_and_multiply(b, d):
+            if d == 0:
+                tiles["gwr", b] = two.tile([P, D, N], F32, tag="gwr", name="gwr")
+                tiles["prod", b] = one.tile([P, D, N], F32, tag="prod", name="prod")
+            gwr, prod = tiles["gwr", b], tiles["prod", b]
+            g_halves = tiles["g_t", b, d // 2][:].bitcast(BF16).rearrange("p (c h) -> p c h", h=2)
+            nc.vector.scalar_tensor_tensor(
+                out=gwr[:, d, :], in0=g_halves[:, :, d % 2], scalar=w_all[:, d : d + 1], in1=tiles["r_t", b][:], op0=MULT, op1=MULT
+            )
+            nc.vector.tensor_tensor(out=prod[:, d, :], in0=gwr[:, d, :], in1=tiles["x_t", b, d][:], op=MULT)
+
+        def channel_sum(terms):
+            sums = psum.tile([P, N], F32, tag="wide")
+            for t in range(PACK):
+                for d in range(D):
+                    flip(sums[:, block_cols(t)], terms[:, d, block_cols(t)], start=(d == 0), stop=(d == D - 1))
+            return sums
+
+        def channel_means(a):
+            s2 = channel_sum(tiles["prod", a])
+            part = one.tile([P, N, D], F32, tag="part")
+            for t in range(PACK):
+                nc.vector.scalar_tensor_tensor(
+                    out=part[:, block_cols(t), :],
+                    in0=tiles["xh", a][:, block_cols(t), :],
+                    scalar=1.0 / D,
+                    in1=s2[:, block_cols(t)].unsqueeze(2).to_broadcast([P, P, D]),
+                    op0=MULT,
+                    op1=MULT,
+                )
+            s1 = channel_sum(tiles["gwr", a])
+            m1 = two.tile([P, N], F32, tag="m1")
+            nc.scalar.mul(out=m1[:], in_=s1[:], mul=1.0 / D)
+            tiles["part", a], tiles["m1", a] = part, m1
+
+        def flip_back(a, d):
+            z_t = psum.tile([P, N], F32, tag="z_t")
+            for t in range(PACK):
+                flip(z_t[:, block_cols(t)], tiles["part", a][:, block_cols(t), d], start=True, stop=False)
+                flip(z_t[:, block_cols(t)], tiles["m1", a][:, block_cols(t)], start=False, stop=True)
+            tiles["z_t", a, d] = z_t
+
+        def finish_dx(a, d):
+            if d == 0:
+                tiles["dx_grouped", a] = one.tile([P, D, P, PACK], BF16, align_bytes=64, tag="dx_grouped", name="dx_grouped")
+            nc.vector.tensor_tensor(
+                out=tiles["dx_grouped", a][:, d, :, :],
+                in0=tiles["gwr", a][:, d, :].rearrange("p (t i) -> p i t", t=PACK),
+                in1=tiles["z_t", a, d][:].rearrange("p (t i) -> p i t", t=PACK),
+                op=SUB,
+            )
+
+        def quantise_dx(a):
+            dx_codes = two.tile([P, D * P], U32, align_bytes=64, tag="dx_codes")
+            dx_scales = two.tile([P, D * P], U8, align_bytes=64, tag="dx_scales")
             nc.vector.quantize_mx(
                 out=dx_codes[:].bitcast(E5M2X4),
                 scales=dx_scales[:],
-                in_=dx_grouped[:].rearrange("p d i t -> p (d i t)"),
+                in_=tiles["dx_grouped", a][:].rearrange("p d i t -> p (d i t)"),
+            )
+            tiles["dx_codes", a], tiles["dx_scales", a] = dx_codes, dx_scales
+
+        def load_and_mask_b(b_pool, kb):
+            b_nat = b_pool.tile([P, N * D], BF16, tag="b_nat")
+            nc.sync.dma_start(out=b_nat[:], in_=b_rows[block_cols(kb), :])
+            mkj = b_pool.tile([P, N], BF16, tag="mkj")
+            nc.sync.dma_start(out=mkj[:], in_=mkj_rows[block_cols(kb), :])
+            tiles["b_nat", kb], tiles["mkj", kb] = b_nat, mkj
+
+        def mask_b(kb):
+            b_3d = tiles["b_nat", kb][:].rearrange("p (j d) -> p j d", d=D)
+            nc.gpsimd.tensor_tensor(out=b_3d, in0=b_3d, in1=tiles["mkj", kb][:].unsqueeze(2).to_broadcast([P, N, D]), op=MULT)
+
+        def flip_b(b_grp, kb, e):
+            if e == 0:
+                tiles["b_grouped", kb] = b_grp.tile([P, D, P, PACK], BF16, align_bytes=64, tag="b_grouped", name="b_grouped")
+            b_words = tiles["b_nat", kb][:].bitcast(F32).rearrange("p (t q e) -> p t e q", t=PACK, e=PAIRS)
+            b_t = psum.tile([P, N], F32, tag="wide")
+            for t in range(PACK):
+                flip(b_t[:, block_cols(t)], b_words[:, t, e, :])
+            nc.scalar.copy(
+                out=tiles["b_grouped", kb][:, 2 * e : 2 * e + 2, :, :],
+                in_=b_t[:].bitcast(BF16).rearrange("p (t k h) -> p h k t", t=PACK, h=2),
             )
 
-            planes = outs.tile([P, D, N], F32)
+        def quantise_b(kb):
             for d in range(D):
-                i_cols = slice(d * P, (d + 1) * P)
-                acc = psum.tile([P, N], F32, tag="acc")
-                nc.tensor.matmul_mx(
-                    out=acc[:],
-                    lhsT=dx_codes[:, i_cols].bitcast(E5M2X4),
-                    lhsT_scale=dx_scales[:, i_cols],
-                    rhs=b_codes[:, d, :].bitcast(E4M3X4),
-                    rhs_scale=b_scales[:, d, :],
-                    start=True,
-                    stop=True,
+                nc.vector.quantize_mx(
+                    out=b_codes[:, d, block_cols(kb)].bitcast(E4M3X4),
+                    scales=b_scales[:, d, block_cols(kb)],
+                    in_=tiles["b_grouped", kb][:, d, :, :].rearrange("p k t -> p (k t)"),
                 )
-                nc.vector.tensor_tensor(out=planes[:, d, :], in0=acc[:], in1=mik[:], op=MULT)
-            out_sb = outs.tile([P, N, D], F32)
-            for half in range(2):
-                d_half = slice(half * 4, half * 4 + 4)
-                nc.scalar.copy(out=out_sb[:, :, d_half], in_=planes[:, d_half, :].rearrange("p d k -> p k d"))
-            nc.sync.dma_start(out=out_rows[i_rows, :], in_=out_sb[:].rearrange("p k d -> p (k d)"))
+
+        def multiply(planes_pool, out_pool, m, d):
+            acc = psum.tile([P, N], F32, tag="wide")
+            nc.tensor.matmul_mx(
+                out=acc[:],
+                lhsT=tiles["dx_codes", m][:, block_cols(d)].bitcast(E5M2X4),
+                lhsT_scale=tiles["dx_scales", m][:, block_cols(d)],
+                rhs=b_codes[:, d, :].bitcast(E4M3X4),
+                rhs_scale=b_scales[:, d, :],
+                start=True,
+                stop=True,
+            )
+            if d % HALF == 0:
+                tiles["planes", m] = planes_pool.tile([P, HALF, N], F32, tag="planes", name="planes")
+            if d == 0:
+                tiles["out_sb", m] = out_pool.tile([P, N, D], F32, tag="out_sb", name="out_sb")
+            nc.scalar.copy(out=tiles["planes", m][:, d % HALF, :], in_=acc[:])
+            if d % HALF == HALF - 1:
+                nc.gpsimd.tensor_tensor(
+                    out=tiles["out_sb", m][:, :, d - HALF + 1 : d + 1],
+                    in0=tiles["planes", m][:].rearrange("p d k -> p k d"),
+                    in1=tiles["mik", m][:].unsqueeze(2).to_broadcast([P, N, HALF]),
+                    op=MULT,
+                )
+            if d == D - 1:
+                nc.sync.dma_start(out=out_rows[block_cols(m), :], in_=tiles["out_sb", m][:].rearrange("p k d -> p (k d)"))
+
+        def dx_slot(slot):
+            b, d = slot // D, slot % D
+            a = b - 1
+            if d == 0 and 0 <= a < BLOCKS:
+                channel_means(a)
+                if b + 1 < BLOCKS:
+                    load_block(b + 1)
+            nxt = slot + 1
+            if nxt // D < BLOCKS:
+                flip_in(nxt // D, nxt % D)
+            if 0 <= a < BLOCKS:
+                flip_back(a, d)
+            if d == HALF and b + 1 < BLOCKS:
+                flip_rstd(b + 1)
+            if b < BLOCKS:
+                scale_and_multiply(b, d)
+            if 0 <= a < BLOCKS:
+                finish_dx(a, d)
+                if d == D - 1:
+                    quantise_dx(a)
+
+        load_block(0)
+        with tc.tile_pool(name="b_pool", bufs=BLOCKS) as b_pool, tc.tile_pool(name="b_grp", bufs=2) as b_grp:
+            load_and_mask_b(b_pool, 0)
+            load_block(1)
+            for kb in range(1, BLOCKS):
+                load_and_mask_b(b_pool, kb)
+            for kb in range(BLOCKS):
+                mask_b(kb)
+            flip_rstd(0)
+            flip_in(0, 0)
+            for slot in range(FIRST_MX_SLOT):
+                dx_slot(slot)
+                kb, turn = (slot - FIRST_B_SLOT) // B_SLOT_STEP, (slot - FIRST_B_SLOT) % B_SLOT_STEP
+                if 0 <= kb < BLOCKS:
+                    if turn < 2:
+                        flip_b(b_grp, kb, 2 * turn)
+                        flip_b(b_grp, kb, 2 * turn + 1)
+                    else:
+                        quantise_b(kb)
+
+        with tc.tile_pool(name="planes_pool", bufs=3) as planes_pool, tc.tile_pool(name="out_pool", bufs=2) as out_pool:
+            for slot in range(FIRST_MX_SLOT, FIRST_MX_SLOT + BLOCKS * D):
+                dx_slot(slot)
+                done = slot - FIRST_MX_SLOT + 1
+                if done % MX_RUN == 0:
+                    for unit in range(done - MX_RUN, done):
+                        multiply(planes_pool, out_pool, unit // D, unit % D)

@@ -64,8 +64,8 @@ def tile_trianglemultiplicativeupdate_pa_v_kernel(
         b_codes = const.tile([P, D, N], U32, align_bytes=64)
         b_scales = const.tile([P, D, N], U8, align_bytes=64)
 
-        def flip(out_cols, in_cols, start=True, stop=True):
-            nc.tensor.matmul(out=out_cols, lhsT=in_cols, rhs=ident[:], is_transpose=True, start=start, stop=stop)
+        def flip(out_cols, in_cols, start=True, stop=True, as_product=False):
+            nc.tensor.matmul(out=out_cols, lhsT=in_cols, rhs=ident[:], is_transpose=not as_product, start=start, stop=stop)
 
         def load_block(b):
             i_rows = block_cols(b)
@@ -96,7 +96,7 @@ def tile_trianglemultiplicativeupdate_pa_v_kernel(
                 tiles["g_t", b, d // 2] = g_t
             x_t = psum.tile([P, N], F32, tag="x_t")
             for t in range(PACK):
-                flip(x_t[:, block_cols(t)], tiles["xh", b][:, block_cols(t), d])
+                flip(x_t[:, block_cols(t)], tiles["xh", b][:, block_cols(t), d], as_product=(t == 0))
             tiles["x_t", b, d] = x_t
 
         def scale_and_multiply(b, d):
@@ -110,15 +110,21 @@ def tile_trianglemultiplicativeupdate_pa_v_kernel(
             )
             nc.vector.tensor_tensor(out=prod[:, d, :], in0=gwr[:, d, :], in1=tiles["x_t", b, d][:], op=MULT)
 
-        def channel_sum(terms):
+        def channel_sum(terms, with_products):
             sums = psum.tile([P, N], F32, tag="wide")
             for t in range(PACK):
                 for d in range(D):
-                    flip(sums[:, block_cols(t)], terms[:, d, block_cols(t)], start=(d == 0), stop=(d == D - 1))
+                    flip(
+                        sums[:, block_cols(t)],
+                        terms[:, d, block_cols(t)],
+                        start=(d == 0),
+                        stop=(d == D - 1),
+                        as_product=(with_products and d == 0),
+                    )
             return sums
 
         def channel_means(a):
-            s2 = channel_sum(tiles["prod", a])
+            s2 = channel_sum(tiles["prod", a], True)
             part = one.tile([P, N, D], F32, tag="part")
             for t in range(PACK):
                 nc.vector.scalar_tensor_tensor(
@@ -129,7 +135,7 @@ def tile_trianglemultiplicativeupdate_pa_v_kernel(
                     op0=MULT,
                     op1=MULT,
                 )
-            s1 = channel_sum(tiles["gwr", a])
+            s1 = channel_sum(tiles["gwr", a], False)
             m1 = two.tile([P, N], F32, tag="m1")
             nc.scalar.mul(out=m1[:], in_=s1[:], mul=1.0 / D)
             tiles["part", a], tiles["m1", a] = part, m1

@@ -64,8 +64,8 @@ def tile_trianglemultiplicativeupdate_pa_v_kernel(
         b_codes = const.tile([P, D, N], U32, align_bytes=64)
         b_scales = const.tile([P, D, N], U8, align_bytes=64)
 
-        def flip(out_cols, in_cols, start=True, stop=True, as_product=False):
-            nc.tensor.matmul(out=out_cols, lhsT=in_cols, rhs=ident[:], is_transpose=not as_product, start=start, stop=stop)
+        def flip(out_cols, in_cols, start=True, stop=True):
+            nc.tensor.matmul(out=out_cols, lhsT=in_cols, rhs=ident[:], is_transpose=True, start=start, stop=stop)
 
         def load_block(b):
             i_rows = block_cols(b)
@@ -96,7 +96,7 @@ def tile_trianglemultiplicativeupdate_pa_v_kernel(
                 tiles["g_t", b, d // 2] = g_t
             x_t = psum.tile([P, N], F32, tag="x_t")
             for t in range(PACK):
-                flip(x_t[:, block_cols(t)], tiles["xh", b][:, block_cols(t), d], as_product=(t == 0))
+                flip(x_t[:, block_cols(t)], tiles["xh", b][:, block_cols(t), d])
             tiles["x_t", b, d] = x_t
 
         def scale_and_multiply(b, d):
@@ -110,21 +110,15 @@ def tile_trianglemultiplicativeupdate_pa_v_kernel(
             )
             nc.vector.tensor_tensor(out=prod[:, d, :], in0=gwr[:, d, :], in1=tiles["x_t", b, d][:], op=MULT)
 
-        def channel_sum(terms, with_products):
+        def channel_sum(terms):
             sums = psum.tile([P, N], F32, tag="wide")
             for t in range(PACK):
                 for d in range(D):
-                    flip(
-                        sums[:, block_cols(t)],
-                        terms[:, d, block_cols(t)],
-                        start=(d == 0),
-                        stop=(d == D - 1),
-                        as_product=(with_products and d == 0),
-                    )
+                    flip(sums[:, block_cols(t)], terms[:, d, block_cols(t)], start=(d == 0), stop=(d == D - 1))
             return sums
 
         def channel_means(a):
-            s2 = channel_sum(tiles["prod", a], True)
+            s2 = channel_sum(tiles["prod", a])
             part = one.tile([P, N, D], F32, tag="part")
             for t in range(PACK):
                 nc.vector.scalar_tensor_tensor(
@@ -135,7 +129,7 @@ def tile_trianglemultiplicativeupdate_pa_v_kernel(
                     op0=MULT,
                     op1=MULT,
                 )
-            s1 = channel_sum(tiles["gwr", a], False)
+            s1 = channel_sum(tiles["gwr", a])
             m1 = two.tile([P, N], F32, tag="m1")
             nc.scalar.mul(out=m1[:], in_=s1[:], mul=1.0 / D)
             tiles["part", a], tiles["m1", a] = part, m1
@@ -198,7 +192,7 @@ def tile_trianglemultiplicativeupdate_pa_v_kernel(
                     in_=tiles["b_grouped", kb][:, d, :, :].rearrange("p k t -> p (k t)"),
                 )
 
-        def multiply(planes_pool, out_pool, m, d):
+        def multiply(m, d):
             acc = psum.tile([P, N], F32, tag="wide")
             nc.tensor.matmul_mx(
                 out=acc[:],
@@ -209,22 +203,26 @@ def tile_trianglemultiplicativeupdate_pa_v_kernel(
                 start=True,
                 stop=True,
             )
+            tiles["acc", m, d] = acc
+
+        def mask_and_store(planes_pool, out_pool, m, d):
             if d % HALF == 0:
                 tiles["planes", m] = planes_pool.tile([P, HALF, N], F32, tag="planes", name="planes")
             if d == 0:
                 tiles["out_sb", m] = out_pool.tile([P, N, D], F32, tag="out_sb", name="out_sb")
-            nc.scalar.copy(out=tiles["planes", m][:, d % HALF, :], in_=acc[:])
+            planes, out_sb = tiles["planes", m], tiles["out_sb", m]
+            nc.vector.tensor_tensor(out=planes[:, d % HALF, :], in0=tiles["acc", m, d][:], in1=tiles["mik", m][:], op=MULT)
             if d % HALF == HALF - 1:
-                nc.gpsimd.tensor_tensor(
-                    out=tiles["out_sb", m][:, :, d - HALF + 1 : d + 1],
-                    in0=tiles["planes", m][:].rearrange("p d k -> p k d"),
-                    in1=tiles["mik", m][:].unsqueeze(2).to_broadcast([P, N, HALF]),
-                    op=MULT,
-                )
-            if d == D - 1:
-                nc.sync.dma_start(out=out_rows[block_cols(m), :], in_=tiles["out_sb", m][:].rearrange("p k d -> p (k d)"))
+                for k_half in range(2):
+                    k_cols = slice(k_half * N // 2, (k_half + 1) * N // 2)
+                    nc.scalar.copy(out=out_sb[:, k_cols, d - HALF + 1 : d + 1], in_=planes[:, :, k_cols].rearrange("p d k -> p k d"))
+                    if d == D - 1:
+                        nc.sync.dma_start(
+                            out=out_rows[block_cols(m), k_half * N * D // 2 : (k_half + 1) * N * D // 2],
+                            in_=out_sb[:, k_cols, :].rearrange("p k d -> p (k d)"),
+                        )
 
-        def dx_slot(slot):
+        def dx_slot(slot, passes):
             b, d = slot // D, slot % D
             a = b - 1
             if d == 0 and 0 <= a < BLOCKS:
@@ -238,6 +236,8 @@ def tile_trianglemultiplicativeupdate_pa_v_kernel(
                 flip_back(a, d)
             if d == HALF and b + 1 < BLOCKS:
                 flip_rstd(b + 1)
+            for unit in passes:
+                multiply(unit // D, unit % D)
             if b < BLOCKS:
                 scale_and_multiply(b, d)
             if 0 <= a < BLOCKS:
@@ -256,7 +256,7 @@ def tile_trianglemultiplicativeupdate_pa_v_kernel(
             flip_rstd(0)
             flip_in(0, 0)
             for slot in range(FIRST_MX_SLOT):
-                dx_slot(slot)
+                dx_slot(slot, [])
                 kb, turn = (slot - FIRST_B_SLOT) // B_SLOT_STEP, (slot - FIRST_B_SLOT) % B_SLOT_STEP
                 if 0 <= kb < BLOCKS:
                     if turn < 2:
@@ -267,8 +267,8 @@ def tile_trianglemultiplicativeupdate_pa_v_kernel(
 
         with tc.tile_pool(name="planes_pool", bufs=3) as planes_pool, tc.tile_pool(name="out_pool", bufs=2) as out_pool:
             for slot in range(FIRST_MX_SLOT, FIRST_MX_SLOT + BLOCKS * D):
-                dx_slot(slot)
                 done = slot - FIRST_MX_SLOT + 1
-                if done % MX_RUN == 0:
-                    for unit in range(done - MX_RUN, done):
-                        multiply(planes_pool, out_pool, unit // D, unit % D)
+                passes = range(done - MX_RUN, done) if done % MX_RUN == 0 else []
+                dx_slot(slot, passes)
+                for unit in passes:
+                    mask_and_store(planes_pool, out_pool, unit // D, unit % D)

@@ -5,25 +5,32 @@ from concourse.masks import make_identity
 
 F32 = mybir.dt.float32
 BF16 = mybir.dt.bfloat16
+I32 = mybir.dt.int32
 U32 = mybir.dt.uint32
 U8 = mybir.dt.uint8
 E4M3X4 = mybir.dt.float8_e4m3fn_x4
 E5M2X4 = mybir.dt.float8_e5m2_x4
 MULT = mybir.AluOpType.mult
-SUB = mybir.AluOpType.subtract
+ADD = mybir.AluOpType.add
+AND = mybir.AluOpType.bitwise_and
+COPY = mybir.ActivationFunctionType.Copy
 
 P = 128
 PACK = 4
 N = 512
 D = 8
-HALF = D // 2
+GROUP = 4
 BLOCKS = N // P
-PAIRS = D // 2
+UNITS = BLOCKS * PACK
+HALF_J = N // 2
+HALVES = UNITS // 2
+PAIRS = BLOCKS * D // 2
+WORDS = D // 2
+B_PARTS = BLOCKS * 2
 
-FIRST_B_SLOT = 9
-B_SLOT_STEP = 3
-FIRST_MX_SLOT = FIRST_B_SLOT + B_SLOT_STEP * BLOCKS
-MX_RUN = 2
+Z_LAG = 6
+FIRST_MX = 10
+SLOTS = UNITS + 9
 
 FLOPS = 2 * D * N * N * N
 BYTES = N * N * D * (2 + 4 + 2 + 4) + N * N * (4 + 2 + 2) + D * 2
@@ -31,6 +38,14 @@ BYTES = N * N * D * (2 + 4 + 2 + 4) + N * N * (4 + 2 + 2) + D * 2
 
 def block_cols(t):
     return slice(t * P, (t + 1) * P)
+
+
+def z_slot(pair):
+    return pair // PACK * PACK + Z_LAG + pair % PACK
+
+
+def mx_slot(pair):
+    return max(z_slot(pair) + 2, FIRST_MX + pair // 2)
 
 
 def tile_trianglemultiplicativeupdate_pa_v_kernel(
@@ -48,9 +63,7 @@ def tile_trianglemultiplicativeupdate_pa_v_kernel(
     with ExitStack() as stack:
         stack.enter_context(tc.manual_schedule())
         const = stack.enter_context(tc.tile_pool(name="const", bufs=1))
-        every = stack.enter_context(tc.tile_pool(name="every", bufs=BLOCKS))
-        two = stack.enter_context(tc.tile_pool(name="two", bufs=2))
-        one = stack.enter_context(tc.tile_pool(name="one", bufs=1))
+        work = stack.enter_context(tc.tile_pool(name="work", bufs=2))
         psum = stack.enter_context(tc.psum_pool(name="psum", bufs=2))
 
         tiles = {}
@@ -67,208 +80,264 @@ def tile_trianglemultiplicativeupdate_pa_v_kernel(
         def flip(out_cols, in_cols, start=True, stop=True):
             nc.tensor.matmul(out=out_cols, lhsT=in_cols, rhs=ident[:], is_transpose=True, start=start, stop=stop)
 
-        def load_block(b):
-            i_rows = block_cols(b)
-            g_nat = two.tile([P, N * D], BF16, tag="g_nat")
-            nc.sync.dma_start(out=g_nat[:], in_=g_rows[i_rows, :])
-            r = two.tile([P, N], F32, tag="r")
-            nc.sync.dma_start(out=r[:], in_=r_rows[i_rows, :])
-            xh = two.tile([P, N, D], F32, tag="xh")
-            nc.sync.dma_start(out=xh[:].rearrange("p j d -> p (j d)"), in_=xh_rows[i_rows, :])
-            mik = every.tile([P, N], BF16, tag="mik")
-            nc.sync.dma_start(out=mik[:], in_=mik_rows[i_rows, :])
-            tiles["g_nat", b], tiles["r", b], tiles["xh", b], tiles["mik", b] = g_nat, r, xh, mik
+        def load_half(h):
+            rows = block_cols(h // 2)
+            cols = slice(h % 2 * HALF_J * D, (h % 2 + 1) * HALF_J * D)
+            g = work.tile([P, HALF_J, D], BF16, tag="g", name="g", bufs=3)
+            nc.sync.dma_start(out=g[:].rearrange("p j d -> p (j d)"), in_=g_rows[rows, cols])
+            xh = work.tile([P, HALF_J, D], F32, tag="xh", name="xh", bufs=4)
+            nc.sync.dma_start(out=xh[:].rearrange("p j d -> p (j d)"), in_=xh_rows[rows, cols])
+            tiles["g", h], tiles["xh", h] = g, xh
+
+        def load_rstd(b):
+            r = work.tile([P, N], F32, tag="r", name="r")
+            nc.sync.dma_start(out=r[:], in_=r_rows[block_cols(b), :])
+            tiles["r", b] = r
+
+        def load_mask_ik(b):
+            mik = work.tile([P, N], BF16, tag="mik", name="mik", bufs=BLOCKS)
+            nc.sync.dma_start(out=mik[:], in_=mik_rows[block_cols(b), :])
+            tiles["mik", b] = mik
+
+        def scale_g(h, channels):
+            if ("gw", h) not in tiles:
+                tiles["gw", h] = work.tile([P, D, HALF_J], F32, tag="gw", name="gw", bufs=6)
+            for d in channels:
+                plane = tiles["gw", h][:, d, :]
+                g_d = tiles["g", h][:, :, d]
+                if d < GROUP:
+                    nc.scalar.activation(out=plane, in_=g_d, func=COPY, scale=w_all[:, d : d + 1])
+                else:
+                    nc.gpsimd.tensor_scalar(out=plane, in0=g_d, scalar1=w_all[:, d : d + 1], scalar2=0.0, op0=MULT, op1=ADD)
+
+        def unit_cols(u):
+            return block_cols(u % 2)
+
+        def multiply_xhat(u):
+            prod = work.tile([P, D, P], F32, tag="prod", name="prod", bufs=3)
+            nc.gpsimd.tensor_tensor(
+                out=prod[:],
+                in0=tiles["gw", u // 2][:, :, unit_cols(u)],
+                in1=tiles["xh", u // 2][:, unit_cols(u), :].rearrange("p q d -> p d q"),
+                op=MULT,
+            )
+            tiles["prod", u] = prod
+
+        def channel_sums(u):
+            bank = psum.tile([P, N], F32, tag="sum", name="sum_ps")
+            for d in range(D):
+                flip(bank[:, block_cols(0)], tiles["prod", u][:, d, :], start=(d == 0), stop=(d == D - 1))
+            for d in range(D):
+                flip(bank[:, block_cols(1)], tiles["gw", u // 2][:, d, unit_cols(u)], start=(d == 0), stop=(d == D - 1))
+            means = work.tile([P, 2 * P], F32, tag="means", name="means")
+            nc.scalar.mul(out=means[:], in_=bank[:, 0 : 2 * P], mul=-1.0 / D)
+            tiles["means", u] = means
+
+        def means_back(u):
+            bank = psum.tile([P, N], F32, tag="nat", name="nat_ps")
+            for half in range(2):
+                flip(bank[:, block_cols(half)], tiles["means", u][:, block_cols(half)])
+            b, t = u // PACK, u % PACK
+            if t == 0:
+                tiles["m1", b] = work.tile([P, N], F32, tag="m1", name="m1")
+            nc.scalar.copy(out=tiles["m1", b][:, block_cols(t)], in_=bank[:, block_cols(1)])
+            tiles["nat", u] = bank
+
+        def multiply_mean(u):
+            part = work.tile([P, D, P], F32, tag="part", name="part", bufs=8)
+            for c in range(0, D, GROUP):
+                nc.vector.tensor_tensor(
+                    out=part[:, c : c + GROUP, :].rearrange("p d q -> p q d"),
+                    in0=tiles["xh", u // 2][:, unit_cols(u), c : c + GROUP],
+                    in1=tiles["nat", u][:, block_cols(0)].unsqueeze(2).to_broadcast([P, P, GROUP]),
+                    op=MULT,
+                )
+            tiles["part", u] = part
 
         def flip_rstd(b):
-            r_ps = psum.tile([P, N], F32, tag="wide")
+            bank = psum.tile([P, N], F32, tag="wide", name="r_ps")
             for t in range(PACK):
-                flip(r_ps[:, block_cols(t)], tiles["r", b][:, block_cols(t)])
-            r_t = two.tile([P, N], F32, tag="r_t")
-            nc.scalar.copy(out=r_t[:], in_=r_ps[:])
+                flip(bank[:, block_cols(t)], tiles["r", b][:, block_cols(t)])
+            r_t = work.tile([P, P, PACK], F32, tag="r_t", name="r_t")
+            nc.scalar.copy(out=r_t[:], in_=bank[:].rearrange("p (t i) -> p i t", t=PACK))
             tiles["r_t", b] = r_t
 
-        def flip_in(b, d):
-            if d % 2 == 0:
-                g_words = tiles["g_nat", b][:].bitcast(F32).rearrange("p (t q e) -> p t e q", t=PACK, e=PAIRS)
-                g_t = psum.tile([P, N], F32, tag="g_t")
+        def finish_dx(pair):
+            b, d0 = pair // PACK, pair % PACK * 2
+            dx = work.tile([P, 2, P, PACK], BF16, align_bytes=64, tag="dx", name="dx", bufs=3)
+            for d in (d0, d0 + 1):
+                bank = psum.tile([P, N], F32, tag="z", name="z_ps")
                 for t in range(PACK):
-                    flip(g_t[:, block_cols(t)], g_words[:, t, d // 2, :])
-                tiles["g_t", b, d // 2] = g_t
-            x_t = psum.tile([P, N], F32, tag="x_t")
-            for t in range(PACK):
-                flip(x_t[:, block_cols(t)], tiles["xh", b][:, block_cols(t), d])
-            tiles["x_t", b, d] = x_t
-
-        def scale_and_multiply(b, d):
-            if d == 0:
-                tiles["gwr", b] = two.tile([P, D, N], F32, tag="gwr", name="gwr")
-                tiles["prod", b] = one.tile([P, D, N], F32, tag="prod", name="prod")
-            gwr, prod = tiles["gwr", b], tiles["prod", b]
-            g_halves = tiles["g_t", b, d // 2][:].bitcast(BF16).rearrange("p (c h) -> p c h", h=2)
-            nc.vector.scalar_tensor_tensor(
-                out=gwr[:, d, :], in0=g_halves[:, :, d % 2], scalar=w_all[:, d : d + 1], in1=tiles["r_t", b][:], op0=MULT, op1=MULT
-            )
-            nc.vector.tensor_tensor(out=prod[:, d, :], in0=gwr[:, d, :], in1=tiles["x_t", b, d][:], op=MULT)
-
-        def channel_sum(terms):
-            sums = psum.tile([P, N], F32, tag="wide")
-            for t in range(PACK):
-                for d in range(D):
-                    flip(sums[:, block_cols(t)], terms[:, d, block_cols(t)], start=(d == 0), stop=(d == D - 1))
-            return sums
-
-        def channel_means(a):
-            s2 = channel_sum(tiles["prod", a])
-            part = one.tile([P, N, D], F32, tag="part")
-            for t in range(PACK):
-                nc.vector.scalar_tensor_tensor(
-                    out=part[:, block_cols(t), :],
-                    in0=tiles["xh", a][:, block_cols(t), :],
-                    scalar=1.0 / D,
-                    in1=s2[:, block_cols(t)].unsqueeze(2).to_broadcast([P, P, D]),
-                    op0=MULT,
-                    op1=MULT,
+                    u = b * PACK + t
+                    cols = bank[:, block_cols(t)]
+                    flip(cols, tiles["gw", u // 2][:, d, unit_cols(u)], start=True, stop=False)
+                    flip(cols, tiles["part", u][:, d, :], start=False, stop=False)
+                    flip(cols, tiles["m1", b][:, block_cols(t)], start=False, stop=True)
+                nc.vector.tensor_tensor(
+                    out=dx[:, d - d0, :, :], in0=bank[:].rearrange("p (t i) -> p i t", t=PACK), in1=tiles["r_t", b][:], op=MULT
                 )
-            s1 = channel_sum(tiles["gwr", a])
-            m1 = two.tile([P, N], F32, tag="m1")
-            nc.scalar.mul(out=m1[:], in_=s1[:], mul=1.0 / D)
-            tiles["part", a], tiles["m1", a] = part, m1
+            tiles["dx", pair] = dx
 
-        def flip_back(a, d):
-            z_t = psum.tile([P, N], F32, tag="z_t")
-            for t in range(PACK):
-                flip(z_t[:, block_cols(t)], tiles["part", a][:, block_cols(t), d], start=True, stop=False)
-                flip(z_t[:, block_cols(t)], tiles["m1", a][:, block_cols(t)], start=False, stop=True)
-            tiles["z_t", a, d] = z_t
-
-        def finish_dx(a, d):
-            if d == 0:
-                tiles["dx_grouped", a] = one.tile([P, D, P, PACK], BF16, align_bytes=64, tag="dx_grouped", name="dx_grouped")
-            nc.vector.tensor_tensor(
-                out=tiles["dx_grouped", a][:, d, :, :],
-                in0=tiles["gwr", a][:, d, :].rearrange("p (t i) -> p i t", t=PACK),
-                in1=tiles["z_t", a, d][:].rearrange("p (t i) -> p i t", t=PACK),
-                op=SUB,
-            )
-
-        def quantise_dx(a):
-            dx_codes = two.tile([P, D * P], U32, align_bytes=64, tag="dx_codes")
-            dx_scales = two.tile([P, D * P], U8, align_bytes=64, tag="dx_scales")
+        def quantise_dx(pair):
+            codes = work.tile([P, 2 * P], U32, align_bytes=64, tag="dx_codes", name="dx_codes", bufs=6)
+            scales = work.tile([P, 2 * P], U8, align_bytes=64, tag="dx_scales", name="dx_scales", bufs=6)
             nc.vector.quantize_mx(
-                out=dx_codes[:].bitcast(E5M2X4),
-                scales=dx_scales[:],
-                in_=tiles["dx_grouped", a][:].rearrange("p d i t -> p (d i t)"),
+                out=codes[:].bitcast(E5M2X4), scales=scales[:], in_=tiles["dx", pair][:].rearrange("p d i t -> p (d i t)")
             )
-            tiles["dx_codes", a], tiles["dx_scales", a] = dx_codes, dx_scales
+            tiles["dx_codes", pair], tiles["dx_scales", pair] = codes, scales
 
-        def load_and_mask_b(b_pool, kb):
-            b_nat = b_pool.tile([P, N * D], BF16, tag="b_nat")
-            nc.sync.dma_start(out=b_nat[:], in_=b_rows[block_cols(kb), :])
-            mkj = b_pool.tile([P, N], BF16, tag="mkj")
+        def load_b(pool, kb):
+            mkj = pool.tile([P, N], BF16, tag="mkj", name="mkj")
             nc.sync.dma_start(out=mkj[:], in_=mkj_rows[block_cols(kb), :])
+            b_nat = pool.tile([P, N * D], BF16, tag="b_nat", name="b_nat")
+            nc.sync.dma_start(out=b_nat[:], in_=b_rows[block_cols(kb), :])
             tiles["b_nat", kb], tiles["mkj", kb] = b_nat, mkj
 
-        def mask_b(kb):
-            b_3d = tiles["b_nat", kb][:].rearrange("p (j d) -> p j d", d=D)
-            nc.gpsimd.tensor_tensor(out=b_3d, in0=b_3d, in1=tiles["mkj", kb][:].unsqueeze(2).to_broadcast([P, N, D]), op=MULT)
-
-        def flip_b(b_grp, kb, e):
-            if e == 0:
-                tiles["b_grouped", kb] = b_grp.tile([P, D, P, PACK], BF16, align_bytes=64, tag="b_grouped", name="b_grouped")
-            b_words = tiles["b_nat", kb][:].bitcast(F32).rearrange("p (t q e) -> p t e q", t=PACK, e=PAIRS)
-            b_t = psum.tile([P, N], F32, tag="wide")
-            for t in range(PACK):
-                flip(b_t[:, block_cols(t)], b_words[:, t, e, :])
-            nc.scalar.copy(
-                out=tiles["b_grouped", kb][:, 2 * e : 2 * e + 2, :, :],
-                in_=b_t[:].bitcast(BF16).rearrange("p (t k h) -> p h k t", t=PACK, h=2),
+        def mask_b(pool, x):
+            kb, w0 = x // 2, x % 2 * 2
+            if w0 == 0:
+                bits = pool.tile([P, N], I32, tag="bits", name="bits")
+                nc.vector.tensor_scalar(out=bits[:], in0=tiles["mkj", kb][:], scalar1=-1.0, scalar2=None, op0=MULT)
+                tiles["bits", kb] = bits
+            b_m = pool.tile([P, 2, N], I32, tag="b_m", name="b_m", bufs=3)
+            nc.vector.tensor_tensor(
+                out=b_m[:].rearrange("p e j -> p j e"),
+                in0=tiles["b_nat", kb][:].bitcast(I32).rearrange("p (j e) -> p j e", e=WORDS)[:, :, w0 : w0 + 2],
+                in1=tiles["bits", kb][:].unsqueeze(2).to_broadcast([P, N, 2]),
+                op=AND,
             )
+            tiles["b_m", x] = b_m
 
-        def quantise_b(kb):
-            for d in range(D):
+        def flip_b(pool, x):
+            b_grp = pool.tile([P, GROUP, P, PACK], BF16, align_bytes=64, tag="b_grp", name="b_grp", bufs=3)
+            words = tiles["b_m", x][:].rearrange("p e j -> p (e j)").bitcast(F32)
+            for e in range(2):
+                bank = psum.tile([P, N], F32, tag="wide", name="b_ps")
+                for t in range(PACK):
+                    flip(bank[:, block_cols(t)], words[:, e * N + t * P : e * N + (t + 1) * P])
+                nc.scalar.copy(
+                    out=b_grp[:, 2 * e : 2 * e + 2, :, :], in_=bank[:].bitcast(BF16).rearrange("p (t k h) -> p h k t", t=PACK, h=2)
+                )
+            tiles["b_grp", x] = b_grp
+
+        def quantise_b(x):
+            kb, d0 = x // 2, x % 2 * GROUP
+            for d in range(GROUP):
                 nc.vector.quantize_mx(
-                    out=b_codes[:, d, block_cols(kb)].bitcast(E4M3X4),
-                    scales=b_scales[:, d, block_cols(kb)],
-                    in_=tiles["b_grouped", kb][:, d, :, :].rearrange("p k t -> p (k t)"),
+                    out=b_codes[:, d0 + d, block_cols(kb)].bitcast(E4M3X4),
+                    scales=b_scales[:, d0 + d, block_cols(kb)],
+                    in_=tiles["b_grp", x][:, d, :, :].rearrange("p k t -> p (k t)"),
                 )
 
-        def multiply(m, d):
-            acc = psum.tile([P, N], F32, tag="wide")
-            nc.tensor.matmul_mx(
-                out=acc[:],
-                lhsT=tiles["dx_codes", m][:, block_cols(d)].bitcast(E5M2X4),
-                lhsT_scale=tiles["dx_scales", m][:, block_cols(d)],
-                rhs=b_codes[:, d, :].bitcast(E4M3X4),
-                rhs_scale=b_scales[:, d, :],
-                start=True,
-                stop=True,
-            )
-            tiles["acc", m, d] = acc
+        def multiply(pair):
+            for c in range(2):
+                d = pair % PACK * 2 + c
+                acc = psum.tile([P, N], F32, tag="wide", name="acc")
+                nc.tensor.matmul_mx(
+                    out=acc[:],
+                    lhsT=tiles["dx_codes", pair][:, block_cols(c)].bitcast(E5M2X4),
+                    lhsT_scale=tiles["dx_scales", pair][:, block_cols(c)],
+                    rhs=b_codes[:, d, :].bitcast(E4M3X4),
+                    rhs_scale=b_scales[:, d, :],
+                    start=True,
+                    stop=True,
+                )
+                tiles["acc", pair, c] = acc
 
-        def mask_and_store(planes_pool, out_pool, m, d):
-            if d % HALF == 0:
-                tiles["planes", m] = planes_pool.tile([P, HALF, N], F32, tag="planes", name="planes")
-            if d == 0:
-                tiles["out_sb", m] = out_pool.tile([P, N, D], F32, tag="out_sb", name="out_sb")
-            planes, out_sb = tiles["planes", m], tiles["out_sb", m]
-            nc.vector.tensor_tensor(out=planes[:, d % HALF, :], in0=tiles["acc", m, d][:], in1=tiles["mik", m][:], op=MULT)
-            if d % HALF == HALF - 1:
-                for k_half in range(2):
-                    k_cols = slice(k_half * N // 2, (k_half + 1) * N // 2)
-                    nc.scalar.copy(out=out_sb[:, k_cols, d - HALF + 1 : d + 1], in_=planes[:, :, k_cols].rearrange("p d k -> p k d"))
-                    if d == D - 1:
-                        nc.sync.dma_start(
-                            out=out_rows[block_cols(m), k_half * N * D // 2 : (k_half + 1) * N * D // 2],
-                            in_=out_sb[:, k_cols, :].rearrange("p k d -> p (k d)"),
-                        )
+        def mask_out(pool, pair):
+            group = pair // 2
+            if pair % 2 == 0:
+                tiles["planes", group] = pool.tile([P, GROUP, N], F32, tag="planes", name="planes")
+            for c in range(2):
+                nc.vector.tensor_tensor(
+                    out=tiles["planes", group][:, pair % 2 * 2 + c, :],
+                    in0=tiles["acc", pair, c][:],
+                    in1=tiles["mik", pair // PACK][:],
+                    op=MULT,
+                )
 
-        def dx_slot(slot, passes):
-            b, d = slot // D, slot % D
-            a = b - 1
-            if d == 0 and 0 <= a < BLOCKS:
-                channel_means(a)
-                if b + 1 < BLOCKS:
-                    load_block(b + 1)
-            nxt = slot + 1
-            if nxt // D < BLOCKS:
-                flip_in(nxt // D, nxt % D)
-            if 0 <= a < BLOCKS:
-                flip_back(a, d)
-            if d == HALF and b + 1 < BLOCKS:
-                flip_rstd(b + 1)
-            for unit in passes:
-                multiply(unit // D, unit % D)
-            if b < BLOCKS:
-                scale_and_multiply(b, d)
-            if 0 <= a < BLOCKS:
-                finish_dx(a, d)
-                if d == D - 1:
-                    quantise_dx(a)
+        def interleave_and_store(pool, group):
+            b, c0 = group // 2, group % 2 * GROUP
+            if c0 == 0:
+                tiles["out_sb", b] = pool.tile([P, N, D], F32, tag="out_sb", name="out_sb")
+            out_sb = tiles["out_sb", b]
+            for k_half in range(2):
+                k_cols = slice(k_half * N // 2, (k_half + 1) * N // 2)
+                nc.scalar.copy(
+                    out=out_sb[:, k_cols, c0 : c0 + GROUP], in_=tiles["planes", group][:, :, k_cols].rearrange("p d k -> p k d")
+                )
+                if c0:
+                    nc.sync.dma_start(
+                        out=out_rows[block_cols(b), k_half * N * D // 2 : (k_half + 1) * N * D // 2],
+                        in_=out_sb[:, k_cols, :].rearrange("p k d -> p (k d)"),
+                    )
 
-        load_block(0)
-        with tc.tile_pool(name="b_pool", bufs=BLOCKS) as b_pool, tc.tile_pool(name="b_grp", bufs=2) as b_grp:
-            load_and_mask_b(b_pool, 0)
-            load_block(1)
-            for kb in range(1, BLOCKS):
-                load_and_mask_b(b_pool, kb)
-            for kb in range(BLOCKS):
-                mask_b(kb)
-            flip_rstd(0)
-            flip_in(0, 0)
-            for slot in range(FIRST_MX_SLOT):
-                dx_slot(slot, [])
-                kb, turn = (slot - FIRST_B_SLOT) // B_SLOT_STEP, (slot - FIRST_B_SLOT) % B_SLOT_STEP
-                if 0 <= kb < BLOCKS:
-                    if turn < 2:
-                        flip_b(b_grp, kb, 2 * turn)
-                        flip_b(b_grp, kb, 2 * turn + 1)
-                    else:
-                        quantise_b(kb)
+        def slot_head(s):
+            if s % 2 == 0 and 4 <= s <= 10:
+                load_half(s // 2 + 2)
+                if s % 4 == 2:
+                    load_rstd(s // 4 + 1)
+            if s == 7:
+                for b in range(BLOCKS):
+                    load_mask_ik(b)
+            if 0 <= s - 2 < UNITS:
+                means_back(s - 2)
+            if 0 <= s - 1 < UNITS:
+                channel_sums(s - 1)
+            for pair in range(PAIRS):
+                if z_slot(pair) == s - 1:
+                    quantise_dx(pair)
 
-        with tc.tile_pool(name="planes_pool", bufs=3) as planes_pool, tc.tile_pool(name="out_pool", bufs=2) as out_pool:
-            for slot in range(FIRST_MX_SLOT, FIRST_MX_SLOT + BLOCKS * D):
-                done = slot - FIRST_MX_SLOT + 1
-                passes = range(done - MX_RUN, done) if done % MX_RUN == 0 else []
-                dx_slot(slot, passes)
-                for unit in passes:
-                    mask_and_store(planes_pool, out_pool, unit // D, unit % D)
+        def slot_middle(s):
+            if 0 <= s - 2 < UNITS:
+                multiply_mean(s - 2)
+            if s < UNITS:
+                multiply_xhat(s)
+                if s // 2 + 1 < HALVES:
+                    for c in range(2):
+                        scale_g(s // 2 + 1, (s % 2 * 2 + c, GROUP + s % 2 * 2 + c))
+
+        def slot_tail(s):
+            if s >= PACK and s % PACK == 0 and s // PACK <= BLOCKS:
+                flip_rstd(s // PACK - 1)
+            for pair in range(PAIRS):
+                if z_slot(pair) == s:
+                    finish_dx(pair)
+            for pair in range(PAIRS):
+                if mx_slot(pair) == s:
+                    multiply(pair)
+
+        with tc.tile_pool(name="b_pool", bufs=2) as b_pool:
+            load_half(0)
+            load_half(1)
+            load_b(b_pool, 0)
+            load_half(2)
+            load_b(b_pool, 1)
+            load_rstd(0)
+            load_rstd(1)
+            scale_g(0, range(D))
+            load_half(3)
+            for s in range(FIRST_MX + 1):
+                if s in (3, 5):
+                    load_b(b_pool, (s + 1) // 2)
+                slot_head(s)
+                if 0 <= s - 3 < B_PARTS:
+                    quantise_b(s - 3)
+                slot_middle(s)
+                if 0 <= s - 1 < B_PARTS:
+                    mask_b(b_pool, s - 1)
+                if 0 <= s - 2 < B_PARTS:
+                    flip_b(b_pool, s - 2)
+                slot_tail(s)
+
+        with tc.tile_pool(name="out_pool", bufs=2) as out_pool:
+            for s in range(FIRST_MX + 1, SLOTS):
+                slot_head(s)
+                done = [pair for pair in range(PAIRS) if mx_slot(pair) == s - 1]
+                for pair in done:
+                    mask_out(out_pool, pair)
+                slot_middle(s)
+                for pair in done:
+                    if pair % 2:
+                        interleave_and_store(out_pool, pair // 2)
+                slot_tail(s)

@@ -11,7 +11,6 @@ U8 = mybir.dt.uint8
 E4M3X4 = mybir.dt.float8_e4m3fn_x4
 E5M2X4 = mybir.dt.float8_e5m2_x4
 MULT = mybir.AluOpType.mult
-ADD = mybir.AluOpType.add
 AND = mybir.AluOpType.bitwise_and
 COPY = mybir.ActivationFunctionType.Copy
 
@@ -29,7 +28,8 @@ WORDS = D // 2
 B_PARTS = BLOCKS * 2
 
 Z_LAG = 6
-FIRST_MX = 10
+B_FIRST = 2
+FIRST_MX = 12
 SLOTS = UNITS + 9
 
 FLOPS = 2 * D * N * N * N
@@ -45,7 +45,7 @@ def z_slot(pair):
 
 
 def mx_slot(pair):
-    return max(z_slot(pair) + 2, FIRST_MX + pair // 2)
+    return max(z_slot(pair) + 1, FIRST_MX + pair * 2 // 3)
 
 
 def tile_trianglemultiplicativeupdate_pa_v_kernel(
@@ -105,22 +105,20 @@ def tile_trianglemultiplicativeupdate_pa_v_kernel(
             for d in channels:
                 plane = tiles["gw", h][:, d, :]
                 g_d = tiles["g", h][:, :, d]
-                if d < GROUP:
-                    nc.scalar.activation(out=plane, in_=g_d, func=COPY, scale=w_all[:, d : d + 1])
-                else:
-                    nc.gpsimd.tensor_scalar(out=plane, in0=g_d, scalar1=w_all[:, d : d + 1], scalar2=0.0, op0=MULT, op1=ADD)
+                nc.scalar.activation(out=plane, in_=g_d, func=COPY, scale=w_all[:, d : d + 1])
 
         def unit_cols(u):
             return block_cols(u % 2)
 
         def multiply_xhat(u):
             prod = work.tile([P, D, P], F32, tag="prod", name="prod", bufs=3)
-            nc.gpsimd.tensor_tensor(
-                out=prod[:],
-                in0=tiles["gw", u // 2][:, :, unit_cols(u)],
-                in1=tiles["xh", u // 2][:, unit_cols(u), :].rearrange("p q d -> p d q"),
-                op=MULT,
-            )
+            for c in range(0, D, GROUP):
+                nc.vector.tensor_tensor(
+                    out=prod[:, c : c + GROUP, :].rearrange("p d q -> p q d"),
+                    in0=tiles["gw", u // 2][:, c : c + GROUP, unit_cols(u)].rearrange("p d q -> p q d"),
+                    in1=tiles["xh", u // 2][:, unit_cols(u), c : c + GROUP],
+                    op=MULT,
+                )
             tiles["prod", u] = prod
 
         def channel_sums(u):
@@ -129,8 +127,11 @@ def tile_trianglemultiplicativeupdate_pa_v_kernel(
                 flip(bank[:, block_cols(0)], tiles["prod", u][:, d, :], start=(d == 0), stop=(d == D - 1))
             for d in range(D):
                 flip(bank[:, block_cols(1)], tiles["gw", u // 2][:, d, unit_cols(u)], start=(d == 0), stop=(d == D - 1))
+            tiles["sums", u] = bank
+
+        def scale_sums(u):
             means = work.tile([P, 2 * P], F32, tag="means", name="means")
-            nc.scalar.mul(out=means[:], in_=bank[:, 0 : 2 * P], mul=-1.0 / D)
+            nc.scalar.mul(out=means[:], in_=tiles["sums", u][:, 0 : 2 * P], mul=-1.0 / D)
             tiles["means", u] = means
 
         def means_back(u):
@@ -155,7 +156,7 @@ def tile_trianglemultiplicativeupdate_pa_v_kernel(
             tiles["part", u] = part
 
         def flip_rstd(b):
-            bank = psum.tile([P, N], F32, tag="wide", name="r_ps")
+            bank = psum.tile([P, N], F32, tag="nat", name="r_ps")
             for t in range(PACK):
                 flip(bank[:, block_cols(t)], tiles["r", b][:, block_cols(t)])
             r_t = work.tile([P, P, PACK], F32, tag="r_t", name="r_t")
@@ -179,8 +180,8 @@ def tile_trianglemultiplicativeupdate_pa_v_kernel(
             tiles["dx", pair] = dx
 
         def quantise_dx(pair):
-            codes = work.tile([P, 2 * P], U32, align_bytes=64, tag="dx_codes", name="dx_codes", bufs=6)
-            scales = work.tile([P, 2 * P], U8, align_bytes=64, tag="dx_scales", name="dx_scales", bufs=6)
+            codes = work.tile([P, 2 * P], U32, align_bytes=64, tag="dx_codes", name="dx_codes", bufs=7)
+            scales = work.tile([P, 2 * P], U8, align_bytes=64, tag="dx_scales", name="dx_scales", bufs=7)
             nc.vector.quantize_mx(
                 out=codes[:].bitcast(E5M2X4), scales=scales[:], in_=tiles["dx", pair][:].rearrange("p d i t -> p (d i t)")
             )
@@ -208,15 +209,20 @@ def tile_trianglemultiplicativeupdate_pa_v_kernel(
             )
             tiles["b_m", x] = b_m
 
-        def flip_b(pool, x):
-            b_grp = pool.tile([P, GROUP, P, PACK], BF16, align_bytes=64, tag="b_grp", name="b_grp", bufs=3)
+        def flip_b(x):
             words = tiles["b_m", x][:].rearrange("p e j -> p (e j)").bitcast(F32)
             for e in range(2):
                 bank = psum.tile([P, N], F32, tag="wide", name="b_ps")
                 for t in range(PACK):
                     flip(bank[:, block_cols(t)], words[:, e * N + t * P : e * N + (t + 1) * P])
+                tiles["b_t", x, e] = bank
+
+        def group_b(pool, x):
+            b_grp = pool.tile([P, GROUP, P, PACK], BF16, align_bytes=64, tag="b_grp", name="b_grp", bufs=3)
+            for e in range(2):
                 nc.scalar.copy(
-                    out=b_grp[:, 2 * e : 2 * e + 2, :, :], in_=bank[:].bitcast(BF16).rearrange("p (t k h) -> p h k t", t=PACK, h=2)
+                    out=b_grp[:, 2 * e : 2 * e + 2, :, :],
+                    in_=tiles["b_t", x, e][:].bitcast(BF16).rearrange("p (t k h) -> p h k t", t=PACK, h=2),
                 )
             tiles["b_grp", x] = b_grp
 
@@ -272,32 +278,46 @@ def tile_trianglemultiplicativeupdate_pa_v_kernel(
                         in_=out_sb[:, k_cols, :].rearrange("p k d -> p (k d)"),
                     )
 
-        def slot_head(s):
+        def slot(s, b_pool, out_pool):
+            done = [pair for pair in range(PAIRS) if mx_slot(pair) == s - 1]
             if s % 2 == 0 and 4 <= s <= 10:
                 load_half(s // 2 + 2)
-                if s % 4 == 2:
-                    load_rstd(s // 4 + 1)
-            if s == 7:
+            if s in (6, 10):
+                load_rstd(s // 4 + 1)
+            if s == 9:
                 for b in range(BLOCKS):
                     load_mask_ik(b)
+            if s in (B_FIRST + 2, B_FIRST + 4):
+                load_b(b_pool, (s - B_FIRST) // 2 + 1)
             if 0 <= s - 2 < UNITS:
                 means_back(s - 2)
             if 0 <= s - 1 < UNITS:
                 channel_sums(s - 1)
+            if 0 <= s - 2 - B_FIRST < B_PARTS:
+                group_b(b_pool, s - 2 - B_FIRST)
             for pair in range(PAIRS):
                 if z_slot(pair) == s - 1:
                     quantise_dx(pair)
-
-        def slot_middle(s):
-            if 0 <= s - 2 < UNITS:
-                multiply_mean(s - 2)
+            if 0 <= s - 3 - B_FIRST < B_PARTS:
+                quantise_b(s - 3 - B_FIRST)
+            for pair in done:
+                mask_out(out_pool, pair)
+            if 0 <= s - B_FIRST < B_PARTS:
+                mask_b(b_pool, s - B_FIRST)
+            if 0 <= s - 1 - B_FIRST < B_PARTS:
+                flip_b(s - 1 - B_FIRST)
             if s < UNITS:
-                multiply_xhat(s)
                 if s // 2 + 1 < HALVES:
                     for c in range(2):
-                        scale_g(s // 2 + 1, (s % 2 * 2 + c, GROUP + s % 2 * 2 + c))
-
-        def slot_tail(s):
+                        scale_g(s // 2 + 1, [d for d in range(D) if d % 2 == s % 2 and d // 4 == c])
+                multiply_xhat(s)
+            if 0 <= s - 1 < UNITS:
+                scale_sums(s - 1)
+            if 0 <= s - 2 < UNITS:
+                multiply_mean(s - 2)
+            for pair in done:
+                if pair % 2:
+                    interleave_and_store(out_pool, pair // 2)
             if s >= PACK and s % PACK == 0 and s // PACK <= BLOCKS:
                 flip_rstd(s // PACK - 1)
             for pair in range(PAIRS):
@@ -310,34 +330,15 @@ def tile_trianglemultiplicativeupdate_pa_v_kernel(
         with tc.tile_pool(name="b_pool", bufs=2) as b_pool:
             load_half(0)
             load_half(1)
-            load_b(b_pool, 0)
             load_half(2)
+            load_b(b_pool, 0)
+            scale_g(0, range(D))
+            load_half(3)
             load_b(b_pool, 1)
             load_rstd(0)
             load_rstd(1)
-            scale_g(0, range(D))
-            load_half(3)
             for s in range(FIRST_MX + 1):
-                if s in (3, 5):
-                    load_b(b_pool, (s + 1) // 2)
-                slot_head(s)
-                if 0 <= s - 3 < B_PARTS:
-                    quantise_b(s - 3)
-                slot_middle(s)
-                if 0 <= s - 1 < B_PARTS:
-                    mask_b(b_pool, s - 1)
-                if 0 <= s - 2 < B_PARTS:
-                    flip_b(b_pool, s - 2)
-                slot_tail(s)
-
+                slot(s, b_pool, None)
         with tc.tile_pool(name="out_pool", bufs=2) as out_pool:
             for s in range(FIRST_MX + 1, SLOTS):
-                slot_head(s)
-                done = [pair for pair in range(PAIRS) if mx_slot(pair) == s - 1]
-                for pair in done:
-                    mask_out(out_pool, pair)
-                slot_middle(s)
-                for pair in done:
-                    if pair % 2:
-                        interleave_and_store(out_pool, pair // 2)
-                slot_tail(s)
+                slot(s, None, out_pool)

@@ -11,6 +11,7 @@ U8 = mybir.dt.uint8
 E4M3X4 = mybir.dt.float8_e4m3fn_x4
 E5M2X4 = mybir.dt.float8_e5m2_x4
 MULT = mybir.AluOpType.mult
+ADD = mybir.AluOpType.add
 AND = mybir.AluOpType.bitwise_and
 COPY = mybir.ActivationFunctionType.Copy
 
@@ -29,8 +30,10 @@ B_PARTS = BLOCKS * 2
 
 Z_LAG = 6
 B_FIRST = 2
-FIRST_MX = 12
-SLOTS = UNITS + 9
+B_RATE = 1
+LOAD_B = [3, 5]
+FIRST_MX = 13
+SLOTS = UNITS + 10
 
 FLOPS = 2 * D * N * N * N
 BYTES = N * N * D * (2 + 4 + 2 + 4) + N * N * (4 + 2 + 2) + D * 2
@@ -45,7 +48,7 @@ def z_slot(pair):
 
 
 def mx_slot(pair):
-    return max(z_slot(pair) + 1, FIRST_MX + pair * 2 // 3)
+    return max(z_slot(pair) + 2, FIRST_MX + pair * 2 // 3)
 
 
 def tile_trianglemultiplicativeupdate_pa_v_kernel(
@@ -107,18 +110,27 @@ def tile_trianglemultiplicativeupdate_pa_v_kernel(
                 g_d = tiles["g", h][:, :, d]
                 nc.scalar.activation(out=plane, in_=g_d, func=COPY, scale=w_all[:, d : d + 1])
 
+        def scale_g_lines(h):
+            tiles["gw", h] = work.tile([P, D, HALF_J], F32, tag="gw", name="gw", bufs=6)
+            for q in range(2):
+                nc.vector.tensor_tensor(
+                    out=tiles["gw", h][:, :, block_cols(q)].rearrange("p (c d) j -> p c j d", c=2),
+                    in0=tiles["g", h][:, block_cols(q), :].rearrange("p j (c d) -> p c j d", c=2),
+                    in1=w_all[:].rearrange("p (c d) -> p c d", c=2).unsqueeze(2).to_broadcast([P, 2, P, GROUP]),
+                    op=MULT,
+                )
+
         def unit_cols(u):
             return block_cols(u % 2)
 
         def multiply_xhat(u):
-            prod = work.tile([P, D, P], F32, tag="prod", name="prod", bufs=3)
-            for c in range(0, D, GROUP):
-                nc.vector.tensor_tensor(
-                    out=prod[:, c : c + GROUP, :].rearrange("p d q -> p q d"),
-                    in0=tiles["gw", u // 2][:, c : c + GROUP, unit_cols(u)].rearrange("p d q -> p q d"),
-                    in1=tiles["xh", u // 2][:, unit_cols(u), c : c + GROUP],
-                    op=MULT,
-                )
+            prod = work.tile([P, D, P], F32, tag="prod", name="prod", bufs=2)
+            nc.vector.tensor_tensor(
+                out=prod[:].rearrange("p (c d) q -> p c q d", c=2),
+                in0=tiles["gw", u // 2][:, :, unit_cols(u)].rearrange("p (c d) q -> p c q d", c=2),
+                in1=tiles["xh", u // 2][:, unit_cols(u), :].rearrange("p q (c d) -> p c q d", c=2),
+                op=MULT,
+            )
             tiles["prod", u] = prod
 
         def channel_sums(u):
@@ -130,18 +142,17 @@ def tile_trianglemultiplicativeupdate_pa_v_kernel(
             tiles["sums", u] = bank
 
         def scale_sums(u):
-            means = work.tile([P, 2 * P], F32, tag="means", name="means")
-            nc.scalar.mul(out=means[:], in_=tiles["sums", u][:, 0 : 2 * P], mul=-1.0 / D)
-            tiles["means", u] = means
-
-        def means_back(u):
-            bank = psum.tile([P, N], F32, tag="nat", name="nat_ps")
-            for half in range(2):
-                flip(bank[:, block_cols(half)], tiles["means", u][:, block_cols(half)])
             b, t = u // PACK, u % PACK
+            m2 = work.tile([P, P], F32, tag="m2", name="m2")
+            nc.scalar.mul(out=m2[:], in_=tiles["sums", u][:, block_cols(0)], mul=-1.0 / D)
             if t == 0:
-                tiles["m1", b] = work.tile([P, N], F32, tag="m1", name="m1")
-            nc.scalar.copy(out=tiles["m1", b][:, block_cols(t)], in_=bank[:, block_cols(1)])
+                tiles["m1", b] = work.tile([P, N], F32, tag="m1", name="m1", bufs=3)
+            nc.scalar.mul(out=tiles["m1", b][:, block_cols(t)], in_=tiles["sums", u][:, block_cols(1)], mul=-1.0 / D)
+            tiles["m2", u] = m2
+
+        def mean_back(u):
+            bank = psum.tile([P, N], F32, tag="nat", name="nat_ps")
+            flip(bank[:, block_cols(0)], tiles["m2", u][:])
             tiles["nat", u] = bank
 
         def multiply_mean(u):
@@ -155,6 +166,31 @@ def tile_trianglemultiplicativeupdate_pa_v_kernel(
                 )
             tiles["part", u] = part
 
+        def add_up(pair):
+            b, d0 = pair // PACK, pair % PACK * 2
+            for d in (d0, d0 + 1):
+                bank = psum.tile([P, N], F32, tag="z", name="z_ps")
+                for t in range(PACK):
+                    u = b * PACK + t
+                    cols = bank[:, block_cols(t)]
+                    flip(cols, tiles["gw", u // 2][:, d, unit_cols(u)], start=True, stop=False)
+                    flip(cols, tiles["part", u][:, d, :], start=False, stop=True)
+                tiles["z", b, d] = bank
+
+        def finish_dx(pair):
+            b, d0 = pair // PACK, pair % PACK * 2
+            dx = work.tile([P, 2, P, PACK], BF16, align_bytes=64, tag="dx", name="dx", bufs=2)
+            for d in (d0, d0 + 1):
+                y = work.tile([P, P, PACK], F32, tag="y", name="y", bufs=2)
+                nc.vector.tensor_tensor(
+                    out=y[:],
+                    in0=tiles["z", b, d][:].rearrange("p (t i) -> p i t", t=PACK),
+                    in1=tiles["m1", b][:].rearrange("p (t i) -> p i t", t=PACK),
+                    op=ADD,
+                )
+                nc.gpsimd.tensor_tensor(out=dx[:, d - d0, :, :], in0=y[:], in1=tiles["r_t", b][:], op=MULT)
+            tiles["dx", pair] = dx
+
         def flip_rstd(b):
             bank = psum.tile([P, N], F32, tag="nat", name="r_ps")
             for t in range(PACK):
@@ -162,22 +198,6 @@ def tile_trianglemultiplicativeupdate_pa_v_kernel(
             r_t = work.tile([P, P, PACK], F32, tag="r_t", name="r_t")
             nc.scalar.copy(out=r_t[:], in_=bank[:].rearrange("p (t i) -> p i t", t=PACK))
             tiles["r_t", b] = r_t
-
-        def finish_dx(pair):
-            b, d0 = pair // PACK, pair % PACK * 2
-            dx = work.tile([P, 2, P, PACK], BF16, align_bytes=64, tag="dx", name="dx", bufs=3)
-            for d in (d0, d0 + 1):
-                bank = psum.tile([P, N], F32, tag="z", name="z_ps")
-                for t in range(PACK):
-                    u = b * PACK + t
-                    cols = bank[:, block_cols(t)]
-                    flip(cols, tiles["gw", u // 2][:, d, unit_cols(u)], start=True, stop=False)
-                    flip(cols, tiles["part", u][:, d, :], start=False, stop=False)
-                    flip(cols, tiles["m1", b][:, block_cols(t)], start=False, stop=True)
-                nc.vector.tensor_tensor(
-                    out=dx[:, d - d0, :, :], in0=bank[:].rearrange("p (t i) -> p i t", t=PACK), in1=tiles["r_t", b][:], op=MULT
-                )
-            tiles["dx", pair] = dx
 
         def quantise_dx(pair):
             codes = work.tile([P, 2 * P], U32, align_bytes=64, tag="dx_codes", name="dx_codes", bufs=7)
@@ -278,51 +298,57 @@ def tile_trianglemultiplicativeupdate_pa_v_kernel(
                         in_=out_sb[:, k_cols, :].rearrange("p k d -> p (k d)"),
                     )
 
+        def b_parts(slot):
+            return [x for x in range(B_PARTS) if x // B_RATE == slot - B_FIRST]
+
         def slot(s, b_pool, out_pool):
-            done = [pair for pair in range(PAIRS) if mx_slot(pair) == s - 1]
-            if s % 2 == 0 and 4 <= s <= 10:
+            if s % 2 and 5 <= s <= 11:
                 load_half(s // 2 + 2)
             if s in (6, 10):
                 load_rstd(s // 4 + 1)
-            if s == 9:
+            if s == 7:
                 for b in range(BLOCKS):
                     load_mask_ik(b)
-            if s in (B_FIRST + 2, B_FIRST + 4):
-                load_b(b_pool, (s - B_FIRST) // 2 + 1)
+            if s in LOAD_B:
+                load_b(b_pool, LOAD_B.index(s) + 2)
             if 0 <= s - 2 < UNITS:
-                means_back(s - 2)
+                mean_back(s - 2)
             if 0 <= s - 1 < UNITS:
                 channel_sums(s - 1)
-            if 0 <= s - 2 - B_FIRST < B_PARTS:
-                group_b(b_pool, s - 2 - B_FIRST)
             for pair in range(PAIRS):
                 if z_slot(pair) == s - 1:
-                    quantise_dx(pair)
-            if 0 <= s - 3 - B_FIRST < B_PARTS:
-                quantise_b(s - 3 - B_FIRST)
-            for pair in done:
-                mask_out(out_pool, pair)
-            if 0 <= s - B_FIRST < B_PARTS:
-                mask_b(b_pool, s - B_FIRST)
-            if 0 <= s - 1 - B_FIRST < B_PARTS:
-                flip_b(s - 1 - B_FIRST)
+                    finish_dx(pair)
+            for pair in range(PAIRS):
+                if mx_slot(pair) == s - 1:
+                    mask_out(out_pool, pair)
+            if 0 <= s - 3 < UNITS:
+                multiply_mean(s - 3)
             if s < UNITS:
-                if s // 2 + 1 < HALVES:
-                    for c in range(2):
-                        scale_g(s // 2 + 1, [d for d in range(D) if d % 2 == s % 2 and d // 4 == c])
                 multiply_xhat(s)
-            if 0 <= s - 1 < UNITS:
-                scale_sums(s - 1)
-            if 0 <= s - 2 < UNITS:
-                multiply_mean(s - 2)
-            for pair in done:
-                if pair % 2:
+            for x in b_parts(s - 2):
+                group_b(b_pool, x)
+            for pair in range(PAIRS):
+                if z_slot(pair) == s - 2:
+                    quantise_dx(pair)
+            for x in b_parts(s - 3):
+                quantise_b(x)
+            for x in b_parts(s):
+                mask_b(b_pool, x)
+            for x in b_parts(s - 1):
+                flip_b(x)
+            if s // 2 + 1 < HALVES:
+                for c in range(2):
+                    scale_g(s // 2 + 1, [d for d in range(D) if d % 2 == s % 2 and d // 4 == c])
+            for pair in range(PAIRS):
+                if mx_slot(pair) == s - 1 and pair % 2:
                     interleave_and_store(out_pool, pair // 2)
             if s >= PACK and s % PACK == 0 and s // PACK <= BLOCKS:
                 flip_rstd(s // PACK - 1)
+            if 0 <= s - 1 < UNITS:
+                scale_sums(s - 1)
             for pair in range(PAIRS):
                 if z_slot(pair) == s:
-                    finish_dx(pair)
+                    add_up(pair)
             for pair in range(PAIRS):
                 if mx_slot(pair) == s:
                     multiply(pair)
@@ -330,13 +356,13 @@ def tile_trianglemultiplicativeupdate_pa_v_kernel(
         with tc.tile_pool(name="b_pool", bufs=2) as b_pool:
             load_half(0)
             load_half(1)
-            load_half(2)
             load_b(b_pool, 0)
-            scale_g(0, range(D))
-            load_half(3)
-            load_b(b_pool, 1)
+            load_half(2)
             load_rstd(0)
             load_rstd(1)
+            scale_g_lines(0)
+            load_half(3)
+            load_b(b_pool, 1)
             for s in range(FIRST_MX + 1):
                 slot(s, b_pool, None)
         with tc.tile_pool(name="out_pool", bufs=2) as out_pool:

@@ -28,12 +28,10 @@ PAIRS = BLOCKS * D // 2
 WORDS = D // 2
 B_PARTS = BLOCKS * 2
 
-Z_LAG = 6
-B_FIRST = 2
-B_RATE = 1
-LOAD_B = [3, 5]
+Z_LAG = 7
+B_FIRST = 3
+LOAD_B = [4, 6]
 FIRST_MX = 13
-SLOTS = UNITS + 10
 
 FLOPS = 2 * D * N * N * N
 BYTES = N * N * D * (2 + 4 + 2 + 4) + N * N * (4 + 2 + 2) + D * 2
@@ -48,7 +46,7 @@ def z_slot(pair):
 
 
 def mx_slot(pair):
-    return max(z_slot(pair) + 2, FIRST_MX + pair * 2 // 3)
+    return FIRST_MX + pair
 
 
 def tile_trianglemultiplicativeupdate_pa_v_kernel(
@@ -133,13 +131,17 @@ def tile_trianglemultiplicativeupdate_pa_v_kernel(
             )
             tiles["prod", u] = prod
 
-        def channel_sums(u):
-            bank = psum.tile([P, N], F32, tag="sum", name="sum_ps")
+        def sum_gw(u):
+            if ("sums", u) not in tiles:
+                tiles["sums", u] = psum.tile([P, N], F32, tag="sum", name="sum_ps")
             for d in range(D):
-                flip(bank[:, block_cols(0)], tiles["prod", u][:, d, :], start=(d == 0), stop=(d == D - 1))
+                flip(tiles["sums", u][:, block_cols(1)], tiles["gw", u // 2][:, d, unit_cols(u)], start=(d == 0), stop=(d == D - 1))
+
+        def sum_prod(u):
+            if ("sums", u) not in tiles:
+                tiles["sums", u] = psum.tile([P, N], F32, tag="sum", name="sum_ps")
             for d in range(D):
-                flip(bank[:, block_cols(1)], tiles["gw", u // 2][:, d, unit_cols(u)], start=(d == 0), stop=(d == D - 1))
-            tiles["sums", u] = bank
+                flip(tiles["sums", u][:, block_cols(0)], tiles["prod", u][:, d, :], start=(d == 0), stop=(d == D - 1))
 
         def scale_sums(u):
             b, t = u // PACK, u % PACK
@@ -298,8 +300,14 @@ def tile_trianglemultiplicativeupdate_pa_v_kernel(
                         in_=out_sb[:, k_cols, :].rearrange("p k d -> p (k d)"),
                     )
 
-        def b_parts(slot):
-            return [x for x in range(B_PARTS) if x // B_RATE == slot - B_FIRST]
+        def b_parts(s):
+            return [x for x in range(B_PARTS) if x + B_FIRST == s]
+
+        def z_pairs(s):
+            return [pair for pair in range(PAIRS) if z_slot(pair) == s]
+
+        def mx_pairs(s):
+            return [pair for pair in range(PAIRS) if mx_slot(pair) == s]
 
         def slot(s, b_pool, out_pool):
             if s % 2 and 5 <= s <= 11:
@@ -311,47 +319,42 @@ def tile_trianglemultiplicativeupdate_pa_v_kernel(
                     load_mask_ik(b)
             if s in LOAD_B:
                 load_b(b_pool, LOAD_B.index(s) + 2)
-            if 0 <= s - 2 < UNITS:
-                mean_back(s - 2)
             if 0 <= s - 1 < UNITS:
-                channel_sums(s - 1)
-            for pair in range(PAIRS):
-                if z_slot(pair) == s - 1:
-                    finish_dx(pair)
-            for pair in range(PAIRS):
-                if mx_slot(pair) == s - 1:
-                    mask_out(out_pool, pair)
+                sum_gw(s - 1)
+                sum_prod(s - 1)
+            for pair in z_pairs(s - 1):
+                finish_dx(pair)
+            for pair in mx_pairs(s - 1):
+                mask_out(out_pool, pair)
             if 0 <= s - 3 < UNITS:
                 multiply_mean(s - 3)
-            if s < UNITS:
-                multiply_xhat(s)
-            for x in b_parts(s - 2):
-                group_b(b_pool, x)
-            for pair in range(PAIRS):
-                if z_slot(pair) == s - 2:
-                    quantise_dx(pair)
-            for x in b_parts(s - 3):
-                quantise_b(x)
             for x in b_parts(s):
                 mask_b(b_pool, x)
+            if s < UNITS:
+                multiply_xhat(s)
+            for pair in z_pairs(s - 2):
+                quantise_dx(pair)
+            for x in b_parts(s - 3):
+                quantise_b(x)
+            for pair in z_pairs(s):
+                add_up(pair)
+            for pair in mx_pairs(s):
+                multiply(pair)
+            if 0 <= s - 2 < UNITS:
+                mean_back(s - 2)
             for x in b_parts(s - 1):
                 flip_b(x)
+            for x in b_parts(s - 2):
+                group_b(b_pool, x)
             if s // 2 + 1 < HALVES:
-                for c in range(2):
-                    scale_g(s // 2 + 1, [d for d in range(D) if d % 2 == s % 2 and d // 4 == c])
-            for pair in range(PAIRS):
-                if mx_slot(pair) == s - 1 and pair % 2:
-                    interleave_and_store(out_pool, pair // 2)
-            if s >= PACK and s % PACK == 0 and s // PACK <= BLOCKS:
-                flip_rstd(s // PACK - 1)
+                scale_g(s // 2 + 1, range(s % 2, D, 2))
             if 0 <= s - 1 < UNITS:
                 scale_sums(s - 1)
-            for pair in range(PAIRS):
-                if z_slot(pair) == s:
-                    add_up(pair)
-            for pair in range(PAIRS):
-                if mx_slot(pair) == s:
-                    multiply(pair)
+            for pair in mx_pairs(s - 1):
+                if pair % 2:
+                    interleave_and_store(out_pool, pair // 2)
+            if s % PACK == 0 and 0 < s // PACK <= BLOCKS:
+                flip_rstd(s // PACK - 1)
 
         with tc.tile_pool(name="b_pool", bufs=2) as b_pool:
             load_half(0)
@@ -366,5 +369,5 @@ def tile_trianglemultiplicativeupdate_pa_v_kernel(
             for s in range(FIRST_MX + 1):
                 slot(s, b_pool, None)
         with tc.tile_pool(name="out_pool", bufs=2) as out_pool:
-            for s in range(FIRST_MX + 1, SLOTS):
+            for s in range(FIRST_MX + 1, mx_slot(PAIRS - 1) + 2):
                 slot(s, None, out_pool)

@@ -81,6 +81,12 @@ def tile_trianglemultiplicativeupdate_pa_v_kernel(
         def flip(out_cols, in_cols, start=True, stop=True):
             nc.tensor.matmul(out=out_cols, lhsT=in_cols, rhs=ident[:], is_transpose=True, start=start, stop=stop)
 
+        def plane_pairs(planes):
+            return planes.rearrange("p d (q e) -> p q d e", e=2)
+
+        def line_pairs(lines):
+            return lines.rearrange("p (q e) d -> p q d e", e=2)
+
         def load_half(h):
             rows = block_cols(h // 2)
             cols = slice(h % 2 * HALF_J * D, (h % 2 + 1) * HALF_J * D)
@@ -123,12 +129,13 @@ def tile_trianglemultiplicativeupdate_pa_v_kernel(
 
         def multiply_xhat(u):
             prod = work.tile([P, D, P], F32, tag="prod", name="prod", bufs=2)
-            nc.vector.tensor_tensor(
-                out=prod[:].rearrange("p (c d) q -> p c q d", c=2),
-                in0=tiles["gw", u // 2][:, :, unit_cols(u)].rearrange("p (c d) q -> p c q d", c=2),
-                in1=tiles["xh", u // 2][:, unit_cols(u), :].rearrange("p q (c d) -> p c q d", c=2),
-                op=MULT,
-            )
+            for c in range(0, D, GROUP):
+                nc.vector.tensor_tensor(
+                    out=plane_pairs(prod[:, c : c + GROUP, :]),
+                    in0=plane_pairs(tiles["gw", u // 2][:, c : c + GROUP, unit_cols(u)]),
+                    in1=line_pairs(tiles["xh", u // 2][:, unit_cols(u), c : c + GROUP]),
+                    op=MULT,
+                )
             tiles["prod", u] = prod
 
         def sum_gw(u):
@@ -161,9 +168,12 @@ def tile_trianglemultiplicativeupdate_pa_v_kernel(
             part = work.tile([P, D, P], F32, tag="part", name="part", bufs=8)
             for c in range(0, D, GROUP):
                 nc.vector.tensor_tensor(
-                    out=part[:, c : c + GROUP, :].rearrange("p d q -> p q d"),
-                    in0=tiles["xh", u // 2][:, unit_cols(u), c : c + GROUP],
-                    in1=tiles["nat", u][:, block_cols(0)].unsqueeze(2).to_broadcast([P, P, GROUP]),
+                    out=plane_pairs(part[:, c : c + GROUP, :]),
+                    in0=line_pairs(tiles["xh", u // 2][:, unit_cols(u), c : c + GROUP]),
+                    in1=tiles["nat", u][:, block_cols(0)]
+                    .rearrange("p (q e) -> p q e", e=2)
+                    .unsqueeze(2)
+                    .to_broadcast([P, P // 2, GROUP, 2]),
                     op=MULT,
                 )
             tiles["part", u] = part
@@ -185,9 +195,9 @@ def tile_trianglemultiplicativeupdate_pa_v_kernel(
             for d in (d0, d0 + 1):
                 y = work.tile([P, P, PACK], F32, tag="y", name="y", bufs=2)
                 nc.vector.tensor_tensor(
-                    out=y[:],
-                    in0=tiles["z", b, d][:].rearrange("p (t i) -> p i t", t=PACK),
-                    in1=tiles["m1", b][:].rearrange("p (t i) -> p i t", t=PACK),
+                    out=line_pairs(y[:]),
+                    in0=plane_pairs(tiles["z", b, d][:].rearrange("p (t i) -> p t i", t=PACK)),
+                    in1=plane_pairs(tiles["m1", b][:].rearrange("p (t i) -> p t i", t=PACK)),
                     op=ADD,
                 )
                 nc.gpsimd.tensor_tensor(out=dx[:, d - d0, :, :], in0=y[:], in1=tiles["r_t", b][:], op=MULT)

@@ -32,6 +32,10 @@ Z_LAG = 7
 B_FIRST = 3
 LOAD_B = [4, 6]
 FIRST_MX = 13
+SINGLE_MX = 3
+MX_LAG = 10
+ROTATE_FROM = 19
+LINE_UNITS = 3
 
 FLOPS = 2 * D * N * N * N
 BYTES = N * N * D * (2 + 4 + 2 + 4) + N * N * (4 + 2 + 2) + D * 2
@@ -42,11 +46,13 @@ def block_cols(t):
 
 
 def z_slot(pair):
-    return pair // PACK * PACK + Z_LAG + pair % PACK
+    return pair + Z_LAG
 
 
 def mx_slot(pair):
-    return FIRST_MX + pair
+    if pair < SINGLE_MX:
+        return FIRST_MX + pair
+    return max(FIRST_MX + SINGLE_MX + (pair - SINGLE_MX) // 2, pair + MX_LAG)
 
 
 def tile_trianglemultiplicativeupdate_pa_v_kernel(
@@ -73,6 +79,8 @@ def tile_trianglemultiplicativeupdate_pa_v_kernel(
         make_identity(nc, ident[:])
         w_bf = const.tile([P, D], BF16)
         nc.scalar.dma_start(out=w_bf[:], in_=ln_out_w.partition_broadcast(P))
+        first = const.tile([P, 1], F32)
+        nc.scalar.activation(out=first[:], in_=ident[:, 0:1], func=COPY)
         w_all = const.tile([P, D], F32)
         nc.vector.tensor_copy(out=w_all[:], in_=w_bf[:])
         b_codes = const.tile([P, D, N], U32, align_bytes=64)
@@ -87,14 +95,24 @@ def tile_trianglemultiplicativeupdate_pa_v_kernel(
         def line_pairs(lines):
             return lines.rearrange("p (q e) d -> p q d e", e=2)
 
-        def load_half(h):
-            rows = block_cols(h // 2)
-            cols = slice(h % 2 * HALF_J * D, (h % 2 + 1) * HALF_J * D)
-            g = work.tile([P, HALF_J, D], BF16, tag="g", name="g", bufs=3)
-            nc.sync.dma_start(out=g[:].rearrange("p j d -> p (j d)"), in_=g_rows[rows, cols])
-            xh = work.tile([P, HALF_J, D], F32, tag="xh", name="xh", bufs=4)
-            nc.sync.dma_start(out=xh[:].rearrange("p j d -> p (j d)"), in_=xh_rows[rows, cols])
-            tiles["g", h], tiles["xh", h] = g, xh
+        def unit_of(rows, u):
+            return rows[block_cols(u // PACK), u % PACK * P * D : (u % PACK + 1) * P * D]
+
+        def load_g(u):
+            g = work.tile([P, P, D], BF16, tag="g", name="g", bufs=4)
+            nc.sync.dma_start(out=g[:].rearrange("p j d -> p (j d)"), in_=unit_of(g_rows, u))
+            tiles["g", u] = g
+
+        def load_g_half(h):
+            g = work.tile([P, HALF_J, D], BF16, tag="g_half", name="g_half", bufs=2)
+            j0 = h % 2 * HALF_J * D
+            nc.sync.dma_start(out=g[:].rearrange("p j d -> p (j d)"), in_=g_rows[block_cols(h // 2), j0 : j0 + HALF_J * D])
+            tiles["g_half", h] = g
+
+        def load_xhat(u):
+            xh = work.tile([P, P, D], F32, tag="xh", name="xh", bufs=7)
+            nc.sync.dma_start(out=xh[:].rearrange("p j d -> p (j d)"), in_=unit_of(xh_rows, u))
+            tiles["xh", u] = xh
 
         def load_rstd(b):
             r = work.tile([P, N], F32, tag="r", name="r")
@@ -106,47 +124,50 @@ def tile_trianglemultiplicativeupdate_pa_v_kernel(
             nc.sync.dma_start(out=mik[:], in_=mik_rows[block_cols(b), :])
             tiles["mik", b] = mik
 
-        def scale_g(h, channels):
-            if ("gw", h) not in tiles:
-                tiles["gw", h] = work.tile([P, D, HALF_J], F32, tag="gw", name="gw", bufs=6)
-            for d in channels:
-                plane = tiles["gw", h][:, d, :]
-                g_d = tiles["g", h][:, :, d]
-                nc.scalar.activation(out=plane, in_=g_d, func=COPY, scale=w_all[:, d : d + 1])
-
-        def scale_g_lines(h):
-            tiles["gw", h] = work.tile([P, D, HALF_J], F32, tag="gw", name="gw", bufs=6)
-            for q in range(2):
-                nc.vector.tensor_tensor(
-                    out=tiles["gw", h][:, :, block_cols(q)].rearrange("p (c d) j -> p c j d", c=2),
-                    in0=tiles["g", h][:, block_cols(q), :].rearrange("p j (c d) -> p c j d", c=2),
-                    in1=w_all[:].rearrange("p (c d) -> p c d", c=2).unsqueeze(2).to_broadcast([P, 2, P, GROUP]),
-                    op=MULT,
-                )
-
         def unit_cols(u):
             return block_cols(u % 2)
 
+        def gw_tile(h):
+            if ("gw", h) not in tiles:
+                tiles["gw", h] = work.tile([P, D, HALF_J], F32, tag="gw", name="gw", bufs=6)
+            return tiles["gw", h]
+
+        def scale_g_lines(u):
+            for c in range(0, D, GROUP):
+                nc.vector.tensor_tensor(
+                    out=plane_pairs(gw_tile(u // 2)[:, c : c + GROUP, unit_cols(u)]),
+                    in0=line_pairs(tiles["g", u][:, :, c : c + GROUP]),
+                    in1=w_all[:, c : c + GROUP].unsqueeze(1).unsqueeze(3).to_broadcast([P, P // 2, GROUP, 2]),
+                    op=MULT,
+                )
+
+        def scale_g_unit(u):
+            for d in range(D):
+                plane = gw_tile(u // 2)[:, d, unit_cols(u)]
+                nc.scalar.activation(out=plane, in_=tiles["g", u][:, :, d], func=COPY, scale=w_all[:, d : d + 1])
+
+        def scale_g_half(h, channels):
+            for d in channels:
+                plane = gw_tile(h)[:, d, :]
+                nc.scalar.activation(out=plane, in_=tiles["g_half", h][:, :, d], func=COPY, scale=w_all[:, d : d + 1])
+
         def multiply_xhat(u):
-            prod = work.tile([P, D, P], F32, tag="prod", name="prod", bufs=2)
+            prod = work.tile([P, D, P], F32, tag="prod", name="prod")
             for c in range(0, D, GROUP):
                 nc.vector.tensor_tensor(
                     out=plane_pairs(prod[:, c : c + GROUP, :]),
                     in0=plane_pairs(tiles["gw", u // 2][:, c : c + GROUP, unit_cols(u)]),
-                    in1=line_pairs(tiles["xh", u // 2][:, unit_cols(u), c : c + GROUP]),
+                    in1=line_pairs(tiles["xh", u][:, :, c : c + GROUP]),
                     op=MULT,
                 )
             tiles["prod", u] = prod
 
         def sum_gw(u):
-            if ("sums", u) not in tiles:
-                tiles["sums", u] = psum.tile([P, N], F32, tag="sum", name="sum_ps")
+            tiles["sums", u] = psum.tile([P, N], F32, tag="sum", name="sum_ps")
             for d in range(D):
                 flip(tiles["sums", u][:, block_cols(1)], tiles["gw", u // 2][:, d, unit_cols(u)], start=(d == 0), stop=(d == D - 1))
 
         def sum_prod(u):
-            if ("sums", u) not in tiles:
-                tiles["sums", u] = psum.tile([P, N], F32, tag="sum", name="sum_ps")
             for d in range(D):
                 flip(tiles["sums", u][:, block_cols(0)], tiles["prod", u][:, d, :], start=(d == 0), stop=(d == D - 1))
 
@@ -169,7 +190,7 @@ def tile_trianglemultiplicativeupdate_pa_v_kernel(
             for c in range(0, D, GROUP):
                 nc.vector.tensor_tensor(
                     out=plane_pairs(part[:, c : c + GROUP, :]),
-                    in0=line_pairs(tiles["xh", u // 2][:, unit_cols(u), c : c + GROUP]),
+                    in0=line_pairs(tiles["xh", u][:, :, c : c + GROUP]),
                     in1=tiles["nat", u][:, block_cols(0)]
                     .rearrange("p (q e) -> p q e", e=2)
                     .unsqueeze(2)
@@ -180,40 +201,41 @@ def tile_trianglemultiplicativeupdate_pa_v_kernel(
 
         def add_up(pair):
             b, d0 = pair // PACK, pair % PACK * 2
-            for d in (d0, d0 + 1):
+            for c in range(2):
                 bank = psum.tile([P, N], F32, tag="z", name="z_ps")
                 for t in range(PACK):
                     u = b * PACK + t
                     cols = bank[:, block_cols(t)]
-                    flip(cols, tiles["gw", u // 2][:, d, unit_cols(u)], start=True, stop=False)
-                    flip(cols, tiles["part", u][:, d, :], start=False, stop=True)
-                tiles["z", b, d] = bank
+                    flip(cols, tiles["gw", u // 2][:, d0 + c, unit_cols(u)], start=True, stop=False)
+                    flip(cols, tiles["part", u][:, d0 + c, :], start=False, stop=True)
+                tiles["z", pair, c] = bank
 
         def finish_dx(pair):
-            b, d0 = pair // PACK, pair % PACK * 2
-            dx = work.tile([P, 2, P, PACK], BF16, align_bytes=64, tag="dx", name="dx", bufs=2)
-            for d in (d0, d0 + 1):
-                y = work.tile([P, P, PACK], F32, tag="y", name="y", bufs=2)
-                nc.vector.tensor_tensor(
-                    out=line_pairs(y[:]),
-                    in0=plane_pairs(tiles["z", b, d][:].rearrange("p (t i) -> p t i", t=PACK)),
-                    in1=plane_pairs(tiles["m1", b][:].rearrange("p (t i) -> p t i", t=PACK)),
-                    op=ADD,
+            b = pair // PACK
+            tag = "dx_last" if b == BLOCKS - 1 and pair % 2 == 0 else "dx"
+            dx = work.tile([P, 2, P, PACK], BF16, align_bytes=64, tag=tag, name="dx", bufs=1)
+            for c in range(2):
+                y = work.tile([P, N], F32, tag="y", name="y", bufs=4)
+                nc.vector.tensor_tensor(out=y[:], in0=tiles["z", pair, c][:], in1=tiles["m1", b][:], op=ADD)
+                nc.gpsimd.tensor_tensor(
+                    out=line_pairs(dx[:, c, :, :]),
+                    in0=plane_pairs(y[:].rearrange("p (t i) -> p t i", t=PACK)),
+                    in1=plane_pairs(tiles["r_t", b][:].rearrange("p (t i) -> p t i", t=PACK)),
+                    op=MULT,
                 )
-                nc.gpsimd.tensor_tensor(out=dx[:, d - d0, :, :], in0=y[:], in1=tiles["r_t", b][:], op=MULT)
             tiles["dx", pair] = dx
 
         def flip_rstd(b):
             bank = psum.tile([P, N], F32, tag="nat", name="r_ps")
             for t in range(PACK):
                 flip(bank[:, block_cols(t)], tiles["r", b][:, block_cols(t)])
-            r_t = work.tile([P, P, PACK], F32, tag="r_t", name="r_t")
-            nc.scalar.copy(out=r_t[:], in_=bank[:].rearrange("p (t i) -> p i t", t=PACK))
+            r_t = work.tile([P, N], F32, tag="r_t", name="r_t")
+            nc.scalar.copy(out=r_t[:], in_=bank[:])
             tiles["r_t", b] = r_t
 
         def quantise_dx(pair):
-            codes = work.tile([P, 2 * P], U32, align_bytes=64, tag="dx_codes", name="dx_codes", bufs=7)
-            scales = work.tile([P, 2 * P], U8, align_bytes=64, tag="dx_scales", name="dx_scales", bufs=7)
+            codes = work.tile([P, 2 * P], U32, align_bytes=64, tag="dx_codes", name="dx_codes", bufs=6)
+            scales = work.tile([P, 2 * P], U8, align_bytes=64, tag="dx_scales", name="dx_scales", bufs=6)
             nc.vector.quantize_mx(
                 out=codes[:].bitcast(E5M2X4), scales=scales[:], in_=tiles["dx", pair][:].rearrange("p d i t -> p (d i t)")
             )
@@ -226,17 +248,18 @@ def tile_trianglemultiplicativeupdate_pa_v_kernel(
             nc.sync.dma_start(out=b_nat[:], in_=b_rows[block_cols(kb), :])
             tiles["b_nat", kb], tiles["mkj", kb] = b_nat, mkj
 
+        def make_bits(pool, kb):
+            bits = pool.tile([P, N], I32, tag="bits", name="bits")
+            nc.gpsimd.tensor_scalar(out=bits[:], in0=tiles["mkj", kb][:], scalar1=-1.0, scalar2=0.0, op0=MULT, op1=ADD)
+            tiles["bits", kb] = bits
+
         def mask_b(pool, x):
             kb, w0 = x // 2, x % 2 * 2
-            if w0 == 0:
-                bits = pool.tile([P, N], I32, tag="bits", name="bits")
-                nc.vector.tensor_scalar(out=bits[:], in0=tiles["mkj", kb][:], scalar1=-1.0, scalar2=None, op0=MULT)
-                tiles["bits", kb] = bits
             b_m = pool.tile([P, 2, N], I32, tag="b_m", name="b_m", bufs=3)
             nc.vector.tensor_tensor(
-                out=b_m[:].rearrange("p e j -> p j e"),
-                in0=tiles["b_nat", kb][:].bitcast(I32).rearrange("p (j e) -> p j e", e=WORDS)[:, :, w0 : w0 + 2],
-                in1=tiles["bits", kb][:].unsqueeze(2).to_broadcast([P, N, 2]),
+                out=plane_pairs(b_m[:]),
+                in0=line_pairs(tiles["b_nat", kb][:].bitcast(I32).rearrange("p (j e) -> p j e", e=WORDS)[:, :, w0 : w0 + 2]),
+                in1=tiles["bits", kb][:].rearrange("p (q e) -> p q e", e=2).unsqueeze(2).to_broadcast([P, N // 2, 2, 2]),
                 op=AND,
             )
             tiles["b_m", x] = b_m
@@ -267,10 +290,13 @@ def tile_trianglemultiplicativeupdate_pa_v_kernel(
                     in_=tiles["b_grp", x][:, d, :, :].rearrange("p k t -> p (k t)"),
                 )
 
+        def acc_tag(pair):
+            return ("wide", "sum", "nat")[pair % 3] if mx_slot(pair) >= ROTATE_FROM else "wide"
+
         def multiply(pair):
             for c in range(2):
                 d = pair % PACK * 2 + c
-                acc = psum.tile([P, N], F32, tag="wide", name="acc")
+                acc = psum.tile([P, N], F32, tag=acc_tag(pair), name="acc")
                 nc.tensor.matmul_mx(
                     out=acc[:],
                     lhsT=tiles["dx_codes", pair][:, block_cols(c)].bitcast(E5M2X4),
@@ -299,15 +325,15 @@ def tile_trianglemultiplicativeupdate_pa_v_kernel(
             if c0 == 0:
                 tiles["out_sb", b] = pool.tile([P, N, D], F32, tag="out_sb", name="out_sb")
             out_sb = tiles["out_sb", b]
-            for k_half in range(2):
-                k_cols = slice(k_half * N // 2, (k_half + 1) * N // 2)
+            cuts = 4 if group == 2 * BLOCKS - 1 else 2
+            for cut in range(cuts):
+                k0, k1 = cut * N // cuts, (cut + 1) * N // cuts
                 nc.scalar.copy(
-                    out=out_sb[:, k_cols, c0 : c0 + GROUP], in_=tiles["planes", group][:, :, k_cols].rearrange("p d k -> p k d")
+                    out=line_pairs(out_sb[:, k0:k1, c0 : c0 + GROUP]), in_=plane_pairs(tiles["planes", group][:, :, k0:k1])
                 )
                 if c0:
                     nc.sync.dma_start(
-                        out=out_rows[block_cols(b), k_half * N * D // 2 : (k_half + 1) * N * D // 2],
-                        in_=out_sb[:, k_cols, :].rearrange("p k d -> p (k d)"),
+                        out=out_rows[block_cols(b), k0 * D : k1 * D], in_=out_sb[:, k0:k1, :].rearrange("p k d -> p (k d)")
                     )
 
         def b_parts(s):
@@ -320,15 +346,20 @@ def tile_trianglemultiplicativeupdate_pa_v_kernel(
             return [pair for pair in range(PAIRS) if mx_slot(pair) == s]
 
         def slot(s, b_pool, out_pool):
-            if s % 2 and 5 <= s <= 11:
-                load_half(s // 2 + 2)
-            if s in (6, 10):
+            if s in (4, 8):
                 load_rstd(s // 4 + 1)
+            if s % 2 and 3 <= s and s // 2 + 3 < HALVES:
+                load_g_half(s // 2 + 3)
+            if 3 <= s < UNITS - 3:
+                load_xhat(s + 3)
             if s == 7:
                 for b in range(BLOCKS):
                     load_mask_ik(b)
             if s in LOAD_B:
                 load_b(b_pool, LOAD_B.index(s) + 2)
+            for x in b_parts(s + 1):
+                if x % 2 == 0:
+                    make_bits(b_pool, x // 2)
             if 0 <= s - 1 < UNITS:
                 sum_gw(s - 1)
                 sum_prod(s - 1)
@@ -338,26 +369,32 @@ def tile_trianglemultiplicativeupdate_pa_v_kernel(
                 mask_out(out_pool, pair)
             if 0 <= s - 3 < UNITS:
                 multiply_mean(s - 3)
-            for x in b_parts(s):
-                mask_b(b_pool, x)
+            if s < LINE_UNITS:
+                scale_g_lines(s)
             if s < UNITS:
                 multiply_xhat(s)
-            for pair in z_pairs(s - 2):
-                quantise_dx(pair)
             for x in b_parts(s - 3):
                 quantise_b(x)
+            for x in b_parts(s):
+                mask_b(b_pool, x)
+            for pair in z_pairs(s - 2):
+                quantise_dx(pair)
             for pair in z_pairs(s):
                 add_up(pair)
-            for pair in mx_pairs(s):
-                multiply(pair)
             if 0 <= s - 2 < UNITS:
                 mean_back(s - 2)
+            for pair in mx_pairs(s)[:1]:
+                multiply(pair)
             for x in b_parts(s - 1):
                 flip_b(x)
+            for pair in mx_pairs(s)[1:]:
+                multiply(pair)
             for x in b_parts(s - 2):
                 group_b(b_pool, x)
-            if s // 2 + 1 < HALVES:
-                scale_g(s // 2 + 1, range(s % 2, D, 2))
+            if s == 0:
+                scale_g_unit(LINE_UNITS)
+            elif s > 1 and s // 2 + 1 < HALVES:
+                scale_g_half(s // 2 + 1, range(s % 2, D, 2))
             if 0 <= s - 1 < UNITS:
                 scale_sums(s - 1)
             for pair in mx_pairs(s - 1):
@@ -367,14 +404,21 @@ def tile_trianglemultiplicativeupdate_pa_v_kernel(
                 flip_rstd(s // PACK - 1)
 
         with tc.tile_pool(name="b_pool", bufs=2) as b_pool:
-            load_half(0)
-            load_half(1)
+            load_g(0)
+            load_xhat(0)
+            load_g(1)
+            load_xhat(1)
+            load_g(3)
+            load_g(2)
+            load_xhat(2)
+            load_g_half(2)
+            load_xhat(3)
             load_b(b_pool, 0)
-            load_half(2)
+            load_xhat(4)
+            load_g_half(3)
             load_rstd(0)
             load_rstd(1)
-            scale_g_lines(0)
-            load_half(3)
+            load_xhat(5)
             load_b(b_pool, 1)
             for s in range(FIRST_MX + 1):
                 slot(s, b_pool, None)

@@ -115,7 +115,7 @@ def tile_trianglemultiplicativeupdate_pa_v_kernel(
             tiles["xh", u] = xh
 
         def load_rstd(b):
-            r = work.tile([P, N], F32, tag="r", name="r")
+            r = work.tile([P, N], F32, tag="r", name="r", bufs=1)
             nc.sync.dma_start(out=r[:], in_=r_rows[block_cols(b), :])
             tiles["r", b] = r
 
@@ -176,9 +176,14 @@ def tile_trianglemultiplicativeupdate_pa_v_kernel(
             m2 = work.tile([P, P], F32, tag="m2", name="m2")
             nc.scalar.mul(out=m2[:], in_=tiles["sums", u][:, block_cols(0)], mul=-1.0 / D)
             if t == 0:
-                tiles["m1", b] = work.tile([P, N], F32, tag="m1", name="m1", bufs=3)
+                tiles["m1", b] = work.tile([P, N], F32, tag="m1", name="m1")
             nc.scalar.mul(out=tiles["m1", b][:, block_cols(t)], in_=tiles["sums", u][:, block_cols(1)], mul=-1.0 / D)
             tiles["m2", u] = m2
+
+        def group_mean(b):
+            m1_lines = work.tile([P, P, PACK], F32, tag="m1_lines", name="m1_lines")
+            nc.scalar.copy(out=line_pairs(m1_lines[:]), in_=plane_pairs(tiles["m1", b][:].rearrange("p (t i) -> p t i", t=PACK)))
+            tiles["m1_lines", b] = m1_lines
 
         def mean_back(u):
             bank = psum.tile([P, N], F32, tag="nat", name="nat_ps")
@@ -215,22 +220,19 @@ def tile_trianglemultiplicativeupdate_pa_v_kernel(
             tag = "dx_last" if b == BLOCKS - 1 and pair % 2 == 0 else "dx"
             dx = work.tile([P, 2, P, PACK], BF16, align_bytes=64, tag=tag, name="dx", bufs=1)
             for c in range(2):
-                y = work.tile([P, N], F32, tag="y", name="y", bufs=4)
-                nc.vector.tensor_tensor(out=y[:], in0=tiles["z", pair, c][:], in1=tiles["m1", b][:], op=ADD)
-                nc.gpsimd.tensor_tensor(
-                    out=line_pairs(dx[:, c, :, :]),
-                    in0=plane_pairs(y[:].rearrange("p (t i) -> p t i", t=PACK)),
-                    in1=plane_pairs(tiles["r_t", b][:].rearrange("p (t i) -> p t i", t=PACK)),
-                    op=MULT,
+                y = work.tile([P, P, PACK], F32, tag="y", name="y", bufs=4)
+                nc.vector.tensor_tensor(
+                    out=y[:], in0=tiles["z", pair, c][:].rearrange("p (t i) -> p i t", t=PACK), in1=tiles["m1_lines", b][:], op=ADD
                 )
+                nc.gpsimd.tensor_tensor(out=dx[:, c, :, :], in0=y[:], in1=tiles["r_t", b][:], op=MULT)
             tiles["dx", pair] = dx
 
         def flip_rstd(b):
             bank = psum.tile([P, N], F32, tag="nat", name="r_ps")
             for t in range(PACK):
                 flip(bank[:, block_cols(t)], tiles["r", b][:, block_cols(t)])
-            r_t = work.tile([P, N], F32, tag="r_t", name="r_t")
-            nc.scalar.copy(out=r_t[:], in_=bank[:])
+            r_t = work.tile([P, P, PACK], F32, tag="r_t", name="r_t")
+            nc.scalar.copy(out=r_t[:], in_=bank[:].rearrange("p (t i) -> p i t", t=PACK))
             tiles["r_t", b] = r_t
 
         def quantise_dx(pair):
@@ -250,7 +252,7 @@ def tile_trianglemultiplicativeupdate_pa_v_kernel(
 
         def make_bits(pool, kb):
             bits = pool.tile([P, N], I32, tag="bits", name="bits")
-            nc.gpsimd.tensor_scalar(out=bits[:], in0=tiles["mkj", kb][:], scalar1=-1.0, scalar2=0.0, op0=MULT, op1=ADD)
+            nc.vector.tensor_scalar(out=bits[:], in0=tiles["mkj", kb][:], scalar1=-1.0, scalar2=None, op0=MULT)
             tiles["bits", kb] = bits
 
         def mask_b(pool, x):
@@ -312,13 +314,16 @@ def tile_trianglemultiplicativeupdate_pa_v_kernel(
             group = pair // 2
             if pair % 2 == 0:
                 tiles["planes", group] = pool.tile([P, GROUP, N], F32, tag="planes", name="planes")
-            for c in range(2):
-                nc.vector.tensor_tensor(
-                    out=tiles["planes", group][:, pair % 2 * 2 + c, :],
-                    in0=tiles["acc", pair, c][:],
-                    in1=tiles["mik", pair // PACK][:],
-                    op=MULT,
-                )
+            cuts = 2 if pair == PAIRS - 1 else 1
+            for cut in range(cuts):
+                cols = slice(cut * N // cuts, (cut + 1) * N // cuts)
+                for c in range(2):
+                    nc.vector.tensor_tensor(
+                        out=tiles["planes", group][:, pair % 2 * 2 + c, cols],
+                        in0=tiles["acc", pair, c][:, cols],
+                        in1=tiles["mik", pair // PACK][:, cols],
+                        op=MULT,
+                    )
 
         def interleave_and_store(pool, group):
             b, c0 = group // 2, group % 2 * GROUP
@@ -328,9 +333,8 @@ def tile_trianglemultiplicativeupdate_pa_v_kernel(
             cuts = 4 if group == 2 * BLOCKS - 1 else 2
             for cut in range(cuts):
                 k0, k1 = cut * N // cuts, (cut + 1) * N // cuts
-                nc.scalar.copy(
-                    out=line_pairs(out_sb[:, k0:k1, c0 : c0 + GROUP]), in_=plane_pairs(tiles["planes", group][:, :, k0:k1])
-                )
+                copy = nc.vector.tensor_copy if cut == 3 else nc.scalar.copy
+                copy(out=line_pairs(out_sb[:, k0:k1, c0 : c0 + GROUP]), in_=plane_pairs(tiles["planes", group][:, :, k0:k1]))
                 if c0:
                     nc.sync.dma_start(
                         out=out_rows[block_cols(b), k0 * D : k1 * D], in_=out_sb[:, k0:k1, :].rearrange("p k d -> p (k d)")
@@ -346,8 +350,8 @@ def tile_trianglemultiplicativeupdate_pa_v_kernel(
             return [pair for pair in range(PAIRS) if mx_slot(pair) == s]
 
         def slot(s, b_pool, out_pool):
-            if s in (4, 8):
-                load_rstd(s // 4 + 1)
+            if s in (5, 9, 13):
+                load_rstd(s // 4)
             if s % 2 and 3 <= s and s // 2 + 3 < HALVES:
                 load_g_half(s // 2 + 3)
             if 3 <= s < UNITS - 3:
@@ -357,9 +361,6 @@ def tile_trianglemultiplicativeupdate_pa_v_kernel(
                     load_mask_ik(b)
             if s in LOAD_B:
                 load_b(b_pool, LOAD_B.index(s) + 2)
-            for x in b_parts(s + 1):
-                if x % 2 == 0:
-                    make_bits(b_pool, x // 2)
             if 0 <= s - 1 < UNITS:
                 sum_gw(s - 1)
                 sum_prod(s - 1)
@@ -377,6 +378,9 @@ def tile_trianglemultiplicativeupdate_pa_v_kernel(
                 quantise_b(x)
             for x in b_parts(s):
                 mask_b(b_pool, x)
+            for x in b_parts(s + 1):
+                if x % 2 == 0:
+                    make_bits(b_pool, x // 2)
             for pair in z_pairs(s - 2):
                 quantise_dx(pair)
             for pair in z_pairs(s):
@@ -402,6 +406,7 @@ def tile_trianglemultiplicativeupdate_pa_v_kernel(
                     interleave_and_store(out_pool, pair // 2)
             if s % PACK == 0 and 0 < s // PACK <= BLOCKS:
                 flip_rstd(s // PACK - 1)
+                group_mean(s // PACK - 1)
 
         with tc.tile_pool(name="b_pool", bufs=2) as b_pool:
             load_g(0)
@@ -417,7 +422,6 @@ def tile_trianglemultiplicativeupdate_pa_v_kernel(
             load_xhat(4)
             load_g_half(3)
             load_rstd(0)
-            load_rstd(1)
             load_xhat(5)
             load_b(b_pool, 1)
             for s in range(FIRST_MX + 1):

@@ -35,6 +35,8 @@ FIRST_MX = 13
 SINGLE_MX = 3
 MX_LAG = 10
 ROTATE_FROM = 19
+FIRST_PRODUCT = 2
+SPARSE_PRODUCTS = 9
 LINE_UNITS = 3
 
 FLOPS = 2 * D * N * N * N
@@ -94,6 +96,9 @@ def tile_trianglemultiplicativeupdate_pa_v_kernel(
 
         def line_pairs(lines):
             return lines.rearrange("p (q e) d -> p q d e", e=2)
+
+        def flip_product(out_cols, in_cols, start, stop):
+            nc.tensor.matmul(out=out_cols, lhsT=in_cols, rhs=ident[:], start=start, stop=stop)
 
         def unit_of(rows, u):
             return rows[block_cols(u // PACK), u % PACK * P * D : (u % PACK + 1) * P * D]
@@ -165,11 +170,13 @@ def tile_trianglemultiplicativeupdate_pa_v_kernel(
         def sum_gw(u):
             tiles["sums", u] = psum.tile([P, N], F32, tag="sum", name="sum_ps")
             for d in range(D):
-                flip(tiles["sums", u][:, block_cols(1)], tiles["gw", u // 2][:, d, unit_cols(u)], start=(d == 0), stop=(d == D - 1))
+                turn = flip_product if d == GROUP and 10 <= u < 14 else flip
+                turn(tiles["sums", u][:, block_cols(1)], tiles["gw", u // 2][:, d, unit_cols(u)], start=(d == 0), stop=(d == D - 1))
 
         def sum_prod(u):
             for d in range(D):
-                flip(tiles["sums", u][:, block_cols(0)], tiles["prod", u][:, d, :], start=(d == 0), stop=(d == D - 1))
+                turn = flip_product if d == GROUP and 10 <= u < 14 else flip
+                turn(tiles["sums", u][:, block_cols(0)], tiles["prod", u][:, d, :], start=(d == 0), stop=(d == D - 1))
 
         def scale_sums(u):
             b, t = u // PACK, u % PACK
@@ -211,7 +218,9 @@ def tile_trianglemultiplicativeupdate_pa_v_kernel(
                 for t in range(PACK):
                     u = b * PACK + t
                     cols = bank[:, block_cols(t)]
-                    flip(cols, tiles["gw", u // 2][:, d0 + c, unit_cols(u)], start=True, stop=False)
+                    product = t in ((1, 3) if pair < SPARSE_PRODUCTS else (2,)) and pair >= FIRST_PRODUCT
+                    turn = flip_product if product else flip
+                    turn(cols, tiles["gw", u // 2][:, d0 + c, unit_cols(u)], start=True, stop=False)
                     flip(cols, tiles["part", u][:, d0 + c, :], start=False, stop=True)
                 tiles["z", pair, c] = bank
 

@@ -32,11 +32,11 @@ Z_LAG = 7
 B_FIRST = 3
 LOAD_B = [4, 6]
 FIRST_MX = 13
-SINGLE_MX = 3
+SINGLE_MX = 4
 MX_LAG = 10
-ROTATE_FROM = 19
+ROTATE_FROM = 18
 FIRST_PRODUCT = 2
-SPARSE_PRODUCTS = 9
+SPARSE_PRODUCTS = 8
 LINE_UNITS = 3
 
 FLOPS = 2 * D * N * N * N
@@ -170,12 +170,12 @@ def tile_trianglemultiplicativeupdate_pa_v_kernel(
         def sum_gw(u):
             tiles["sums", u] = psum.tile([P, N], F32, tag="sum", name="sum_ps")
             for d in range(D):
-                turn = flip_product if d == GROUP and 10 <= u < 14 else flip
+                turn = flip_product if d == GROUP and 9 <= u < 14 else flip
                 turn(tiles["sums", u][:, block_cols(1)], tiles["gw", u // 2][:, d, unit_cols(u)], start=(d == 0), stop=(d == D - 1))
 
         def sum_prod(u):
             for d in range(D):
-                turn = flip_product if d == GROUP and 10 <= u < 14 else flip
+                turn = flip_product if d == GROUP and 9 <= u < 14 else flip
                 turn(tiles["sums", u][:, block_cols(0)], tiles["prod", u][:, d, :], start=(d == 0), stop=(d == D - 1))
 
         def scale_sums(u):
@@ -218,7 +218,7 @@ def tile_trianglemultiplicativeupdate_pa_v_kernel(
                 for t in range(PACK):
                     u = b * PACK + t
                     cols = bank[:, block_cols(t)]
-                    product = t in ((1, 3) if pair < SPARSE_PRODUCTS else (2,)) and pair >= FIRST_PRODUCT
+                    product = t in ((1, 3) if pair < SPARSE_PRODUCTS else (0,)) and pair >= FIRST_PRODUCT
                     turn = flip_product if product else flip
                     turn(cols, tiles["gw", u // 2][:, d0 + c, unit_cols(u)], start=True, stop=False)
                     flip(cols, tiles["part", u][:, d0 + c, :], start=False, stop=True)

from contextlib import ExitStack

import concourse.mybir as mybir
from concourse.masks import make_identity

F32 = mybir.dt.float32
BF16 = mybir.dt.bfloat16
I32 = mybir.dt.int32
U32 = mybir.dt.uint32
U8 = mybir.dt.uint8
E4M3X4 = mybir.dt.float8_e4m3fn_x4
E5M2X4 = mybir.dt.float8_e5m2_x4
MULT = mybir.AluOpType.mult
ADD = mybir.AluOpType.add
AND = mybir.AluOpType.bitwise_and
COPY = mybir.ActivationFunctionType.Copy

P = 128
PACK = 4
N = 512
D = 8
GROUP = 4
BLOCKS = N // P
UNITS = BLOCKS * PACK
HALF_J = N // 2
HALVES = UNITS // 2
PAIRS = BLOCKS * D // 2
WORDS = D // 2
B_PARTS = BLOCKS * 2

Z_LAG = 7
B_FIRST = 3
LOAD_B = [4, 6]
FIRST_MX = 13
SINGLE_MX = 4
MX_LAG = 10
ROTATE_FROM = 18
FIRST_PRODUCT = 2
SPARSE_PRODUCTS = 8
LINE_UNITS = 3

FLOPS = 2 * D * N * N * N
BYTES = N * N * D * (2 + 4 + 2 + 4) + N * N * (4 + 2 + 2) + D * 2


def block_cols(t):
    return slice(t * P, (t + 1) * P)


def z_slot(pair):
    return pair + Z_LAG


def mx_slot(pair):
    if pair < SINGLE_MX:
        return FIRST_MX + pair
    return max(FIRST_MX + SINGLE_MX + (pair - SINGLE_MX) // 2, pair + MX_LAG)


def tile_trianglemultiplicativeupdate_pa_v_kernel(
    tc, a_gated, b_gated, mask_ik, mask_kj, ln_out_w, ln_out_b, xhat, rstd, grad_out, out
):
    nc = tc.nc
    b_rows = b_gated.rearrange("n k j d -> (n k) (j d)")
    g_rows = grad_out.rearrange("n i j d -> (n i) (j d)")
    xh_rows = xhat.rearrange("n i j d -> (n i) (j d)")
    out_rows = out.rearrange("n i k d -> (n i) (k d)")
    r_rows = rstd.rearrange("n i j -> (n i) j")
    mik_rows = mask_ik.rearrange("n i k -> (n i) k")
    mkj_rows = mask_kj.rearrange("n k j -> (n k) j")

    with ExitStack() as stack:
        stack.enter_context(tc.manual_schedule())
        const = stack.enter_context(tc.tile_pool(name="const", bufs=1))
        work = stack.enter_context(tc.tile_pool(name="work", bufs=2))
        psum = stack.enter_context(tc.psum_pool(name="psum", bufs=2))

        tiles = {}

        ident = const.tile([P, P], F32)
        make_identity(nc, ident[:])
        w_bf = const.tile([P, D], BF16)
        nc.scalar.dma_start(out=w_bf[:], in_=ln_out_w.partition_broadcast(P))
        first = const.tile([P, 1], F32)
        nc.scalar.activation(out=first[:], in_=ident[:, 0:1], func=COPY)
        w_all = const.tile([P, D], F32)
        nc.vector.tensor_copy(out=w_all[:], in_=w_bf[:])
        b_codes = const.tile([P, D, N], U32, align_bytes=64)
        b_scales = const.tile([P, D, N], U8, align_bytes=64)

        def flip(out_cols, in_cols, start=True, stop=True):
            nc.tensor.matmul(out=out_cols, lhsT=in_cols, rhs=ident[:], is_transpose=True, start=start, stop=stop)

        def plane_pairs(planes):
            return planes.rearrange("p d (q e) -> p q d e", e=2)

        def line_pairs(lines):
            return lines.rearrange("p (q e) d -> p q d e", e=2)

        def flip_product(out_cols, in_cols, start, stop):
            nc.tensor.matmul(out=out_cols, lhsT=in_cols, rhs=ident[:], start=start, stop=stop)

        def unit_of(rows, u):
            return rows[block_cols(u // PACK), u % PACK * P * D : (u % PACK + 1) * P * D]

        def load_g(u):
            g = work.tile([P, P, D], BF16, tag="g", name="g", bufs=4)
            nc.sync.dma_start(out=g[:].rearrange("p j d -> p (j d)"), in_=unit_of(g_rows, u))
            tiles["g", u] = g

        def load_g_half(h):
            g = work.tile([P, HALF_J, D], BF16, tag="g_half", name="g_half", bufs=2)
            j0 = h % 2 * HALF_J * D
            nc.sync.dma_start(out=g[:].rearrange("p j d -> p (j d)"), in_=g_rows[block_cols(h // 2), j0 : j0 + HALF_J * D])
            tiles["g_half", h] = g

        def load_xhat(u):
            xh = work.tile([P, P, D], F32, tag="xh", name="xh", bufs=7)
            nc.sync.dma_start(out=xh[:].rearrange("p j d -> p (j d)"), in_=unit_of(xh_rows, u))
            tiles["xh", u] = xh

        def load_rstd(b):
            r = work.tile([P, N], F32, tag="r", name="r", bufs=1)
            nc.sync.dma_start(out=r[:], in_=r_rows[block_cols(b), :])
            tiles["r", b] = r

        def load_mask_ik(b):
            mik = work.tile([P, N], BF16, tag="mik", name="mik", bufs=BLOCKS)
            nc.sync.dma_start(out=mik[:], in_=mik_rows[block_cols(b), :])
            tiles["mik", b] = mik

        def unit_cols(u):
            return block_cols(u % 2)

        def gw_tile(h):
            if ("gw", h) not in tiles:
                tiles["gw", h] = work.tile([P, D, HALF_J], F32, tag="gw", name="gw", bufs=6)
            return tiles["gw", h]

        def scale_g_lines(u):
            for c in range(0, D, GROUP):
                nc.vector.tensor_tensor(
                    out=plane_pairs(gw_tile(u // 2)[:, c : c + GROUP, unit_cols(u)]),
                    in0=line_pairs(tiles["g", u][:, :, c : c + GROUP]),
                    in1=w_all[:, c : c + GROUP].unsqueeze(1).unsqueeze(3).to_broadcast([P, P // 2, GROUP, 2]),
                    op=MULT,
                )

        def scale_g_unit(u):
            for d in range(D):
                plane = gw_tile(u // 2)[:, d, unit_cols(u)]
                nc.scalar.activation(out=plane, in_=tiles["g", u][:, :, d], func=COPY, scale=w_all[:, d : d + 1])

        def scale_g_half(h, channels):
            for d in channels:
                plane = gw_tile(h)[:, d, :]
                nc.scalar.activation(out=plane, in_=tiles["g_half", h][:, :, d], func=COPY, scale=w_all[:, d : d + 1])

        def multiply_xhat(u):
            prod = work.tile([P, D, P], F32, tag="prod", name="prod")
            for c in range(0, D, GROUP):
                nc.vector.tensor_tensor(
                    out=plane_pairs(prod[:, c : c + GROUP, :]),
                    in0=plane_pairs(tiles["gw", u // 2][:, c : c + GROUP, unit_cols(u)]),
                    in1=line_pairs(tiles["xh", u][:, :, c : c + GROUP]),
                    op=MULT,
                )
            tiles["prod", u] = prod

        def sum_gw(u):
            tiles["sums", u] = psum.tile([P, N], F32, tag="sum", name="sum_ps")
            for d in range(D):
                turn = flip_product if d == GROUP and 9 <= u < 14 else flip
                turn(tiles["sums", u][:, block_cols(1)], tiles["gw", u // 2][:, d, unit_cols(u)], start=(d == 0), stop=(d == D - 1))

        def sum_prod(u):
            for d in range(D):
                turn = flip_product if d == GROUP and 9 <= u < 14 else flip
                turn(tiles["sums", u][:, block_cols(0)], tiles["prod", u][:, d, :], start=(d == 0), stop=(d == D - 1))

        def scale_sums(u):
            b, t = u // PACK, u % PACK
            m2 = work.tile([P, P], F32, tag="m2", name="m2")
            nc.scalar.mul(out=m2[:], in_=tiles["sums", u][:, block_cols(0)], mul=-1.0 / D)
            if t == 0:
                tiles["m1", b] = work.tile([P, N], F32, tag="m1", name="m1")
            nc.scalar.mul(out=tiles["m1", b][:, block_cols(t)], in_=tiles["sums", u][:, block_cols(1)], mul=-1.0 / D)
            tiles["m2", u] = m2

        def group_mean(b):
            m1_lines = work.tile([P, P, PACK], F32, tag="m1_lines", name="m1_lines")
            nc.scalar.copy(out=line_pairs(m1_lines[:]), in_=plane_pairs(tiles["m1", b][:].rearrange("p (t i) -> p t i", t=PACK)))
            tiles["m1_lines", b] = m1_lines

        def mean_back(u):
            bank = psum.tile([P, N], F32, tag="nat", name="nat_ps")
            flip(bank[:, block_cols(0)], tiles["m2", u][:])
            tiles["nat", u] = bank

        def multiply_mean(u):
            part = work.tile([P, D, P], F32, tag="part", name="part", bufs=8)
            for c in range(0, D, GROUP):
                nc.vector.tensor_tensor(
                    out=plane_pairs(part[:, c : c + GROUP, :]),
                    in0=line_pairs(tiles["xh", u][:, :, c : c + GROUP]),
                    in1=tiles["nat", u][:, block_cols(0)]
                    .rearrange("p (q e) -> p q e", e=2)
                    .unsqueeze(2)
                    .to_broadcast([P, P // 2, GROUP, 2]),
                    op=MULT,
                )
            tiles["part", u] = part

        def add_up(pair):
            b, d0 = pair // PACK, pair % PACK * 2
            for c in range(2):
                bank = psum.tile([P, N], F32, tag="z", name="z_ps")
                for t in range(PACK):
                    u = b * PACK + t
                    cols = bank[:, block_cols(t)]
                    product = t in ((1, 3) if pair < SPARSE_PRODUCTS else (0,)) and pair >= FIRST_PRODUCT
                    turn = flip_product if product else flip
                    turn(cols, tiles["gw", u // 2][:, d0 + c, unit_cols(u)], start=True, stop=False)
                    flip(cols, tiles["part", u][:, d0 + c, :], start=False, stop=True)
                tiles["z", pair, c] = bank

        def finish_dx(pair):
            b = pair // PACK
            tag = "dx_last" if b == BLOCKS - 1 and pair % 2 == 0 else "dx"
            dx = work.tile([P, 2, P, PACK], BF16, align_bytes=64, tag=tag, name="dx", bufs=1)
            for c in range(2):
                y = work.tile([P, P, PACK], F32, tag="y", name="y", bufs=4)
                nc.vector.tensor_tensor(
                    out=y[:], in0=tiles["z", pair, c][:].rearrange("p (t i) -> p i t", t=PACK), in1=tiles["m1_lines", b][:], op=ADD
                )
                nc.gpsimd.tensor_tensor(out=dx[:, c, :, :], in0=y[:], in1=tiles["r_t", b][:], op=MULT)
            tiles["dx", pair] = dx

        def flip_rstd(b):
            bank = psum.tile([P, N], F32, tag="nat", name="r_ps")
            for t in range(PACK):
                flip(bank[:, block_cols(t)], tiles["r", b][:, block_cols(t)])
            r_t = work.tile([P, P, PACK], F32, tag="r_t", name="r_t")
            nc.scalar.copy(out=r_t[:], in_=bank[:].rearrange("p (t i) -> p i t", t=PACK))
            tiles["r_t", b] = r_t

        def quantise_dx(pair):
            codes = work.tile([P, 2 * P], U32, align_bytes=64, tag="dx_codes", name="dx_codes", bufs=6)
            scales = work.tile([P, 2 * P], U8, align_bytes=64, tag="dx_scales", name="dx_scales", bufs=6)
            nc.vector.quantize_mx(
                out=codes[:].bitcast(E5M2X4), scales=scales[:], in_=tiles["dx", pair][:].rearrange("p d i t -> p (d i t)")
            )
            tiles["dx_codes", pair], tiles["dx_scales", pair] = codes, scales

        def load_b(pool, kb):
            mkj = pool.tile([P, N], BF16, tag="mkj", name="mkj")
            nc.sync.dma_start(out=mkj[:], in_=mkj_rows[block_cols(kb), :])
            b_nat = pool.tile([P, N * D], BF16, tag="b_nat", name="b_nat")
            nc.sync.dma_start(out=b_nat[:], in_=b_rows[block_cols(kb), :])
            tiles["b_nat", kb], tiles["mkj", kb] = b_nat, mkj

        def make_bits(pool, kb):
            bits = pool.tile([P, N], I32, tag="bits", name="bits")
            nc.vector.tensor_scalar(out=bits[:], in0=tiles["mkj", kb][:], scalar1=-1.0, scalar2=None, op0=MULT)
            tiles["bits", kb] = bits

        def mask_b(pool, x):
            kb, w0 = x // 2, x % 2 * 2
            b_m = pool.tile([P, 2, N], I32, tag="b_m", name="b_m", bufs=3)
            nc.vector.tensor_tensor(
                out=plane_pairs(b_m[:]),
                in0=line_pairs(tiles["b_nat", kb][:].bitcast(I32).rearrange("p (j e) -> p j e", e=WORDS)[:, :, w0 : w0 + 2]),
                in1=tiles["bits", kb][:].rearrange("p (q e) -> p q e", e=2).unsqueeze(2).to_broadcast([P, N // 2, 2, 2]),
                op=AND,
            )
            tiles["b_m", x] = b_m

        def flip_b(x):
            words = tiles["b_m", x][:].rearrange("p e j -> p (e j)").bitcast(F32)
            for e in range(2):
                bank = psum.tile([P, N], F32, tag="wide", name="b_ps")
                for t in range(PACK):
                    flip(bank[:, block_cols(t)], words[:, e * N + t * P : e * N + (t + 1) * P])
                tiles["b_t", x, e] = bank

        def group_b(pool, x):
            b_grp = pool.tile([P, GROUP, P, PACK], BF16, align_bytes=64, tag="b_grp", name="b_grp", bufs=3)
            for e in range(2):
                nc.scalar.copy(
                    out=b_grp[:, 2 * e : 2 * e + 2, :, :],
                    in_=tiles["b_t", x, e][:].bitcast(BF16).rearrange("p (t k h) -> p h k t", t=PACK, h=2),
                )
            tiles["b_grp", x] = b_grp

        def quantise_b(x):
            kb, d0 = x // 2, x % 2 * GROUP
            for d in range(GROUP):
                nc.vector.quantize_mx(
                    out=b_codes[:, d0 + d, block_cols(kb)].bitcast(E4M3X4),
                    scales=b_scales[:, d0 + d, block_cols(kb)],
                    in_=tiles["b_grp", x][:, d, :, :].rearrange("p k t -> p (k t)"),
                )

        def acc_tag(pair):
            return ("wide", "sum", "nat")[pair % 3] if mx_slot(pair) >= ROTATE_FROM else "wide"

        def multiply(pair):
            for c in range(2):
                d = pair % PACK * 2 + c
                acc = psum.tile([P, N], F32, tag=acc_tag(pair), name="acc")
                nc.tensor.matmul_mx(
                    out=acc[:],
                    lhsT=tiles["dx_codes", pair][:, block_cols(c)].bitcast(E5M2X4),
                    lhsT_scale=tiles["dx_scales", pair][:, block_cols(c)],
                    rhs=b_codes[:, d, :].bitcast(E4M3X4),
                    rhs_scale=b_scales[:, d, :],
                    start=True,
                    stop=True,
                )
                tiles["acc", pair, c] = acc

        def mask_out(pool, pair):
            group = pair // 2
            if pair % 2 == 0:
                tiles["planes", group] = pool.tile([P, GROUP, N], F32, tag="planes", name="planes")
            cuts = 2 if pair == PAIRS - 1 else 1
            for cut in range(cuts):
                cols = slice(cut * N // cuts, (cut + 1) * N // cuts)
                for c in range(2):
                    nc.vector.tensor_tensor(
                        out=tiles["planes", group][:, pair % 2 * 2 + c, cols],
                        in0=tiles["acc", pair, c][:, cols],
                        in1=tiles["mik", pair // PACK][:, cols],
                        op=MULT,
                    )

        def interleave_and_store(pool, group):
            b, c0 = group // 2, group % 2 * GROUP
            if c0 == 0:
                tiles["out_sb", b] = pool.tile([P, N, D], F32, tag="out_sb", name="out_sb")
            out_sb = tiles["out_sb", b]
            cuts = 4 if group == 2 * BLOCKS - 1 else 2
            for cut in range(cuts):
                k0, k1 = cut * N // cuts, (cut + 1) * N // cuts
                copy = nc.vector.tensor_copy if cut == 3 else nc.scalar.copy
                copy(out=line_pairs(out_sb[:, k0:k1, c0 : c0 + GROUP]), in_=plane_pairs(tiles["planes", group][:, :, k0:k1]))
                if c0:
                    nc.sync.dma_start(
                        out=out_rows[block_cols(b), k0 * D : k1 * D], in_=out_sb[:, k0:k1, :].rearrange("p k d -> p (k d)")
                    )

        def b_parts(s):
            return [x for x in range(B_PARTS) if x + B_FIRST == s]

        def z_pairs(s):
            return [pair for pair in range(PAIRS) if z_slot(pair) == s]

        def mx_pairs(s):
            return [pair for pair in range(PAIRS) if mx_slot(pair) == s]

        def slot(s, b_pool, out_pool):
            if s in (5, 9, 13):
                load_rstd(s // 4)
            if s % 2 and 3 <= s and s // 2 + 3 < HALVES:
                load_g_half(s // 2 + 3)
            if 3 <= s < UNITS - 3:
                load_xhat(s + 3)
            if s == 7:
                for b in range(BLOCKS):
                    load_mask_ik(b)
            if s in LOAD_B:
                load_b(b_pool, LOAD_B.index(s) + 2)
            if 0 <= s - 1 < UNITS:
                sum_gw(s - 1)
                sum_prod(s - 1)
            for pair in z_pairs(s - 1):
                finish_dx(pair)
            for pair in mx_pairs(s - 1):
                mask_out(out_pool, pair)
            if 0 <= s - 3 < UNITS:
                multiply_mean(s - 3)
            if s < LINE_UNITS:
                scale_g_lines(s)
            if s < UNITS:
                multiply_xhat(s)
            for x in b_parts(s - 3):
                quantise_b(x)
            for x in b_parts(s):
                mask_b(b_pool, x)
            for x in b_parts(s + 1):
                if x % 2 == 0:
                    make_bits(b_pool, x // 2)
            for pair in z_pairs(s - 2):
                quantise_dx(pair)
            for pair in z_pairs(s):
                add_up(pair)
            if 0 <= s - 2 < UNITS:
                mean_back(s - 2)
            for pair in mx_pairs(s)[:1]:
                multiply(pair)
            for x in b_parts(s - 1):
                flip_b(x)
            for pair in mx_pairs(s)[1:]:
                multiply(pair)
            for x in b_parts(s - 2):
                group_b(b_pool, x)
            if s == 0:
                scale_g_unit(LINE_UNITS)
            elif s > 1 and s // 2 + 1 < HALVES:
                scale_g_half(s // 2 + 1, range(s % 2, D, 2))
            if 0 <= s - 1 < UNITS:
                scale_sums(s - 1)
            for pair in mx_pairs(s - 1):
                if pair % 2:
                    interleave_and_store(out_pool, pair // 2)
            if s % PACK == 0 and 0 < s // PACK <= BLOCKS:
                flip_rstd(s // PACK - 1)
                group_mean(s // PACK - 1)

        with tc.tile_pool(name="b_pool", bufs=2) as b_pool:
            load_g(0)
            load_xhat(0)
            load_g(1)
            load_xhat(1)
            load_g(3)
            load_g(2)
            load_xhat(2)
            load_g_half(2)
            load_xhat(3)
            load_b(b_pool, 0)
            load_xhat(4)
            load_g_half(3)
            load_rstd(0)
            load_xhat(5)
            load_b(b_pool, 1)
            for s in range(FIRST_MX + 1):
                slot(s, b_pool, None)
        with tc.tile_pool(name="out_pool", bufs=2) as out_pool:
            for s in range(FIRST_MX + 1, mx_slot(PAIRS - 1) + 2):
                slot(s, None, out_pool)
